import numpy as np
import ml_dtypes


def mxq(x, axis, fmt="e4m3"):
    dtype, down = {"e4m3": (ml_dtypes.float8_e4m3fn, 7), "e5m2": (ml_dtypes.float8_e5m2, 14)}[fmt]
    v = np.moveaxis(np.asarray(x, np.float32).astype(ml_dtypes.bfloat16).astype(np.float64), axis, -1)
    blocks = v.reshape(v.shape[:-1] + (-1, 32))
    amax = np.abs(blocks).max(-1, keepdims=True)
    byte = np.maximum(np.where(amax > 0, np.frexp(amax)[1] - 1 + 127, 0) - down, 1)
    scale = np.exp2(byte - 127.0)
    codes = (blocks / scale).astype(np.float32).astype(dtype).astype(np.float64)
    return np.moveaxis((codes * scale).reshape(v.shape), -1, axis)


WIDE = False


def mx_kscale(k):
    if not WIDE:
        return np.ones(k)
    levels = np.array([10, -10, 5, -5, 0])
    if k % 512:
        return np.exp2(np.random.permutation(np.resize(levels, k // 32))).repeat(32)
    a = np.empty((k // 512, 16))
    for p in range(k // 512):
        a[p, :8] = np.random.permutation(np.resize(levels, 8))
        for g in range(8):
            far = levels[np.abs(levels - a[p, g]) >= 10]
            a[p, g + 8] = far[np.random.randint(len(far))]
    return np.exp2(a.ravel()).repeat(32)


BF16 = ml_dtypes.bfloat16


def bf(x):
    return np.asarray(x, np.float32).astype(BF16)


def f64(x):
    return np.asarray(x).astype(np.float64)


B, S, DIM, H, HD = 4, 128, 2048, 16, 128
E = H * HD


def rope_tables():
    inv_freq = 1.0 / (10000.0 ** (np.arange(0, HD, 2) / HD))
    freqs = np.outer(np.arange(S), inv_freq)
    emb = np.concatenate([freqs, freqs], axis=-1)
    return np.cos(emb)[None, None], np.sin(emb)[None, None]


def rotate_half(x):
    x1, x2 = np.split(x, 2, axis=-1)
    return np.concatenate([-x2, x1], axis=-1)


def draw0():
    s = mx_kscale(DIM)
    cos, sin = rope_tables()
    return {"key_value": bf(np.random.standard_normal((B, S, DIM)) * s),
            "wk": bf(np.random.standard_normal((E, DIM)) / np.sqrt(DIM) / s),
            "bk": bf(np.random.standard_normal(E) * 0.1),
            "wv": bf(np.random.standard_normal((E, DIM)) / np.sqrt(DIM) / s),
            "bv": bf(np.random.standard_normal(E) * 0.1),
            "cos": bf(cos), "sin": bf(sin)}


def core(key_value, wk, bk, wv, bv, cos, sin):
    xq = mxq(f64(key_value), 2, "e4m3")
    k = (xq @ mxq(f64(wk), 1, "e4m3").T) + f64(bk)
    v = (xq @ mxq(f64(wv), 1, "e4m3").T) + f64(bv)
    k = k.reshape(B, S, H, HD).transpose(0, 2, 1, 3)
    v = v.reshape(B, S, H, HD).transpose(0, 2, 1, 3)
    k = k * f64(cos) + rotate_half(k) * f64(sin)
    return k, v


def e4m3fn_bytes(y):
    return np.clip(np.asarray(y, np.float64), -448.0, 448.0).astype(np.float32).astype(ml_dtypes.float8_e4m3fn).view(np.uint8)


def e4m3fn_values(b):
    return np.asarray(b, np.uint8).view(ml_dtypes.float8_e4m3fn).astype(np.float64)


def setup_inputs():
    d = draw0()
    x0 = np.asarray(d['wv']).astype(np.float64)
    s = (np.max(np.abs(x0), axis=(0,), keepdims=True) / 448.0).astype(np.float32)
    out = {}
    for k, v in d.items():
        if k == 'wv':
            out['wv_bytes'] = e4m3fn_bytes(x0 / s.astype(np.float64))
            out['wv_scale'] = s
        else:
            out[k] = v
    return out


def reference(key_value, wk, bk, wv_bytes, wv_scale, bv, cos, sin):
    return core(key_value, wk, bk, e4m3fn_values(wv_bytes) * wv_scale.astype(np.float64), bv, cos, sin)

@@ -1,0 +1,295 @@
+from contextlib import ExitStack
+
+import concourse.mybir as mybir
+from concourse.masks import make_identity
+
+F32 = mybir.dt.float32
+BF16 = mybir.dt.bfloat16
+U32 = mybir.dt.uint32
+U8 = mybir.dt.uint8
+FP8 = mybir.dt.float8_e4m3fn
+FP8X4 = mybir.dt.float8_e4m3fn_x4
+ALU = mybir.AluOpType
+
+NB, S, DIM, H, HD = 4, 128, 2048, 16, 128
+P = 128
+G = DIM // 512
+TOK = NB * S
+FLOPS = 2 * TOK * DIM * 2 * H * HD
+
+
+def tile_attention_pb_kernel(tc, key_value, wk, bk, wv_bytes, wv_scale, bv, cos, sin, out_0, out_1):
+    nc = tc.nc
+    with ExitStack() as ctx:
+        const = ctx.enter_context(tc.tile_pool(name="const", bufs=1))
+        raw = ctx.enter_context(tc.tile_pool(name="raw", bufs=5))
+        vby = ctx.enter_context(tc.tile_pool(name="vby", bufs=4))
+        vbf = ctx.enter_context(tc.tile_pool(name="vbf", bufs=4))
+        prm = ctx.enter_context(tc.tile_pool(name="prm", bufs=3))
+        grp = ctx.enter_context(tc.tile_pool(name="grp", bufs=3))
+        cod = ctx.enter_context(tc.tile_pool(name="cod", bufs=3))
+        rot = ctx.enter_context(tc.tile_pool(name="rot", bufs=4))
+        fins = ctx.enter_context(tc.tile_pool(name="fins", bufs=6))
+        psum = ctx.enter_context(tc.psum_pool(name="psum", bufs=2))
+        ctx.enter_context(tc.manual_schedule())
+
+        units = [("v", 0), ("k", 0)]
+        for i in range(1, 8):
+            units.append(("k", i))
+            units.append(("v", i))
+        n_units = len(units)
+        LOOKAHEAD = 5
+        FIRST_ORDERED = 4
+
+        s_raw = const.tile([P, P], F32, name="s_raw")
+        nc.gpsimd.memset(s_raw[:], 0.0)
+        b_raw = const.tile([P, P], BF16, name="b_raw")
+        nc.gpsimd.memset(b_raw[:], 0.0)
+        ident = const.tile([P, P], F32, name="ident")
+        make_identity(nc, ident[:])
+        cs_raw = const.tile([P, 2, P], BF16, name="cs_raw")
+        nc.sync.dma_start(out=s_raw[0:16, :], in_=wv_scale.rearrange("o (m p) -> (o m) p", p=P))
+        nc.sync.dma_start(out=cs_raw[:, 0, :], in_=cos.rearrange("a b s d -> (a b s) d"))
+        nc.sync.dma_start(out=cs_raw[:, 1, :], in_=sin.rearrange("a b s d -> (a b s) d"))
+        nc.sync.dma_start(out=b_raw[0:H, :], in_=bk.rearrange("(h d) -> h d", d=HD))
+
+        scale_b = const.tile([P, DIM], F32, name="scale_b")
+        bv_b = const.tile([P, H * HD], BF16, name="bv_b")
+
+        src = {}
+        byt = {}
+        rawk = {}
+
+        def load(idx):
+            kind, i = units[idx]
+            rows = slice(256 * i, 256 * (i + 1))
+            if kind == "k":
+                t = raw.tile([P, 2, DIM], BF16, tag="raw", name="wkr%d" % i)
+                nc.sync.dma_start(out=t[:], in_=wk[rows, :].rearrange("(r p) k -> p r k", p=P))
+                rawk[idx] = t
+            else:
+                t = vby.tile([P, 2, DIM], U8, tag="vby", name="wvy%d" % i)
+                nc.sync.dma_start(out=t[:], in_=wv_bytes[rows, :].rearrange("(r p) k -> p r k", p=P))
+                byt[idx] = t
+
+        load(0)
+        xr = []
+        for j in range(2):
+            xr_t = raw.tile([P, 2, DIM], BF16, tag="raw", name="xr%d" % j)
+            xr.append(xr_t)
+        for b in range(NB):
+            nc.sync.dma_start(out=xr[b // 2][:, b % 2, :], in_=key_value[b])
+        load(3)
+        load(1)
+        load(2)
+        nc.sync.dma_start(out=bv_b[:], in_=bv.partition_broadcast(P))
+        load(4)
+
+        perm = const.tile([P, P], F32, name="perm")
+        nc.vector.tensor_copy(out=perm[:, 0:64], in_=ident[:, 64:128])
+        nc.vector.tensor_copy(out=perm[:, 64:128], in_=ident[:, 0:64])
+        csf = const.tile([P, 2, P], F32, name="csf")
+        nc.vector.tensor_copy(out=csf[:, 0, :], in_=cs_raw[:, 0, :])
+        nc.vector.tensor_copy(out=csf[:, 1, 0:64], in_=cs_raw[:, 1, 64:128])
+        nc.vector.tensor_scalar(out=csf[:, 1, 64:128], in0=cs_raw[:, 1, 0:64], scalar1=-1.0, scalar2=None, op0=ALU.mult)
+        b_f = const.tile([P, P], F32, name="b_f")
+        nc.vector.tensor_copy(out=b_f[:], in_=b_raw[:])
+
+        scol = const.tile([P, 16], F32, name="scol")
+        tp0 = psum.tile([P, NB, S], F32, tag="tp", bufs=4, name="tp0")
+        nc.tensor.transpose(tp0[:, 0, :], s_raw[:], ident[:])
+        nc.scalar.copy(out=scol[:], in_=tp0[:, 0, 0:16])
+        for q in range(4):
+            tpq = psum.tile([P, 4, P], F32, tag="tp", bufs=4, name="tpq")
+            for mm in range(4):
+                m = 4 * q + mm
+                nc.tensor.transpose(tpq[:, mm, :], scol[:, m : m + 1].to_broadcast([P, P]), ident[:])
+            nc.vector.tensor_copy(out=scale_b[:, 512 * q : 512 * (q + 1)], in_=tpq[:].rearrange("p m r -> p (m r)"))
+
+        x_codes = const.tile([P, G, TOK], U32, name="x_codes", align_bytes=64)
+        x_scales = const.tile([P, G, TOK], U8, name="x_scales", align_bytes=64)
+
+        codes = {}
+        rots = {}
+        groups = {}
+
+        def product(idx, r):
+            if r == 0:
+                t = vbf.tile([P, 2, DIM], BF16, tag="vbf", name="wvb%d" % idx)
+                src[idx] = t
+            nc.vector.tensor_tensor(out=src[idx][:, r, :], in0=byt[idx][:, r, :].bitcast(FP8), in1=scale_b[:], op=ALU.mult)
+
+        pieces = []
+        for idx in range(n_units):
+            if units[idx][0] == "v":
+                pieces.append((idx, 0))
+                pieces.append((idx, 1))
+
+        def next_products(count):
+            for c in range(count):
+                if len(pieces) > 0:
+                    idx, r = pieces.pop(0)
+                    product(idx, r)
+
+        def permute(idx):
+            t = prm.tile([P, 2, G, 2, P], F32, tag="prm", name="wkp%d" % idx)
+            src[idx] = t
+            for r in range(2):
+                nc.scalar.copy(out=t[:, r, :, :, :], in_=rawk[idx][:, r, :].bitcast(F32).rearrange("p (g j u) -> p g u j", g=G, u=2))
+
+        def turn(idx):
+            wg = grp.tile([P, G, 256, 4], BF16, tag="grp", name="wg%d" % idx, align_bytes=64)
+            groups[idx] = wg
+            for r in range(2):
+                for gp in range(2):
+                    tp = psum.tile([P, 2, 2, P], F32, tag="tp", bufs=4, name="tpw")
+                    for gg in range(2):
+                        g = 2 * gp + gg
+                        for u in range(2):
+                            if units[idx][0] == "k" and idx >= FIRST_ORDERED:
+                                nc.tensor.transpose(tp[:, gg, u, :], src[idx][:, r, g, u, :], ident[:])
+                            else:
+                                rows = rawk[idx] if units[idx][0] == "k" else src[idx]
+                                words = rows[:, r, :].bitcast(F32)
+                                nc.tensor.transpose(tp[:, gg, u, :], words[:, 256 * g + u : 256 * (g + 1) : 2], ident[:])
+                    nc.scalar.copy(out=wg[:, 2 * gp : 2 * gp + 2, r * P : (r + 1) * P, :].bitcast(F32), in_=tp[:].rearrange("p g u c -> p g c u"))
+
+        def quantise(idx):
+            wc = cod.tile([P, G * 256], U32, tag="wc", name="wc%d" % idx, align_bytes=64)
+            ws = cod.tile([P, G * 256], U8, tag="ws", name="ws%d" % idx, align_bytes=64)
+            nc.vector.quantize_mx(out=wc[:].bitcast(FP8X4), scales=ws[:], in_=groups[idx][:].rearrange("p g c t -> p (g c t)"))
+            codes[idx] = (wc, ws)
+
+        def multiply_k(idx):
+            i = units[idx][1]
+            wc, ws = codes[idx]
+            pair = []
+            for r in range(2):
+                h = 2 * i + r
+                acc = psum.tile([P, TOK], F32, tag="acc", bufs=2, name="acck")
+                for g in range(G):
+                    cols = slice(g * 256 + r * P, g * 256 + (r + 1) * P)
+                    nc.tensor.matmul_mx(
+                        out=acc[:],
+                        lhsT=wc[:, cols].bitcast(FP8X4),
+                        lhsT_scale=ws[:, cols],
+                        rhs=x_codes[:, g, :].bitcast(FP8X4),
+                        rhs_scale=x_scales[:, g, :],
+                        start=(g == 0),
+                        stop=(g == G - 1),
+                    )
+                rab = rot.tile([P, 2, TOK], F32, tag="rab", name="rab%d" % h)
+                nc.vector.scalar_tensor_tensor(
+                    out=rab[:],
+                    in0=acc[:].unsqueeze(1).to_broadcast([P, 2, TOK]),
+                    scalar=bias_t[:, h : h + 1],
+                    in1=cs2[:].rearrange("p c b s -> p c (b s)"),
+                    op0=ALU.add,
+                    op1=ALU.mult,
+                )
+                pair.append(rab)
+            rots[idx] = pair
+
+        def back_k(idx):
+            i = units[idx][1]
+            for r in range(2):
+                h = 2 * i + r
+                rab = rots[idx][r]
+                ob = psum.tile([P, NB, HD], F32, tag="ob", bufs=2, name="ob")
+                for b in range(NB):
+                    cols = slice(b * S, (b + 1) * S)
+                    nc.tensor.matmul(ob[:, b, :], lhsT=rab[:, 0, cols], rhs=ident[:], is_transpose=True, start=True, stop=False)
+                    nc.tensor.matmul(ob[:, b, :], lhsT=rab[:, 1, cols], rhs=perm[:], is_transpose=True, start=False, stop=True)
+                fin = fins.tile([P, NB, HD], F32, tag="fin", name="fink")
+                nc.scalar.copy(out=fin[:], in_=ob[:])
+                nc.sync.dma_start(out=out_0[:, h, :, :].rearrange("b s d -> s b d"), in_=fin[:])
+
+        def multiply_v(idx, halves):
+            i = units[idx][1]
+            wc, ws = codes[idx]
+            for bp in halves:
+                acc = psum.tile([P, 2, 256], F32, tag="acc", bufs=2, name="accv")
+                for bb in range(2):
+                    b = 2 * bp + bb
+                    for g in range(G):
+                        nc.tensor.matmul_mx(
+                            out=acc[:, bb, :],
+                            lhsT=x_codes[:, g, b * S : (b + 1) * S].bitcast(FP8X4),
+                            lhsT_scale=x_scales[:, g, b * S : (b + 1) * S],
+                            rhs=wc[:, g * 256 : (g + 1) * 256].bitcast(FP8X4),
+                            rhs_scale=ws[:, g * 256 : (g + 1) * 256],
+                            start=(g == 0),
+                            stop=(g == G - 1),
+                        )
+                fin = fins.tile([P, 2, 256], F32, tag="fin", name="finv")
+                nc.vector.tensor_tensor(
+                    out=fin[:],
+                    in0=acc[:],
+                    in1=bv_b[:, 256 * i : 256 * (i + 1)].unsqueeze(1).to_broadcast([P, 2, 256]),
+                    op=ALU.add,
+                )
+                for bb in range(2):
+                    b = 2 * bp + bb
+                    nc.sync.dma_start(
+                        out=out_1[b, 2 * i : 2 * i + 2, :, :].rearrange("h s d -> s h d"),
+                        in_=fin[:, bb, :].rearrange("p (h d) -> p h d", d=HD),
+                    )
+
+        next_products(2)
+
+        xg = []
+        for gp in range(2):
+            xg_t = grp.tile([P, 2, TOK, 4], BF16, tag="grp", name="xg%d" % gp, align_bytes=64)
+            xg.append(xg_t)
+        for b in range(NB):
+            words = xr[b // 2][:, b % 2, :].bitcast(F32)
+            for gp in range(2):
+                tp = psum.tile([P, 2, 2, P], F32, tag="tp", bufs=4, name="tpx")
+                for gg in range(2):
+                    g = 2 * gp + gg
+                    for u in range(2):
+                        nc.tensor.transpose(tp[:, gg, u, :], words[:, 256 * g + u : 256 * (g + 1) : 2], ident[:])
+                dst = xg[gp][:, :, b * P : (b + 1) * P, :].bitcast(F32)
+                nc.scalar.copy(out=dst, in_=tp[:].rearrange("p g u c -> p g c u"))
+        for gp in range(2):
+            nc.vector.quantize_mx(
+                out=x_codes[:, 2 * gp : 2 * gp + 2, :].rearrange("p g c -> p (g c)").bitcast(FP8X4),
+                scales=x_scales[:, 2 * gp : 2 * gp + 2, :].rearrange("p g c -> p (g c)"),
+                in_=xg[gp][:].rearrange("p g c t -> p (g c t)"),
+            )
+
+        turn(0)
+        quantise(0)
+
+        cst = const.tile([P, 3, P], F32, name="cst")
+        tpc = psum.tile([P, 4, P], F32, tag="tp", bufs=4, name="tpc")
+        nc.tensor.transpose(tpc[:, 0, :], csf[:, 0, :], ident[:])
+        nc.tensor.transpose(tpc[:, 1, :], csf[:, 1, :], ident[:])
+        nc.tensor.transpose(tpc[:, 2, :], b_f[:], ident[:])
+        nc.scalar.copy(out=cst[:], in_=tpc[:, 0:3, :])
+        bias_t = cst[:, 2, :]
+        cs2 = const.tile([P, 2, NB, S], F32, name="cs2")
+
+        for j in range(n_units):
+            if j + LOOKAHEAD < n_units:
+                load(j + LOOKAHEAD)
+            next_products(1)
+            if j + 1 < n_units:
+                turn(j + 1)
+            if j == 0:
+                nc.scalar.copy(out=cs2[:], in_=cst[:, 0:2, :].unsqueeze(2).to_broadcast([P, 2, NB, S]))
+            if j + 2 < n_units and units[j + 2][0] == "k" and j + 2 >= FIRST_ORDERED:
+                permute(j + 2)
+            if j + 1 < n_units:
+                quantise(j + 1)
+            if j == n_units - 1:
+                multiply_v(j, (0,))
+                back_k(j - 1)
+                multiply_v(j, (1,))
+            else:
+                if j >= 2 and units[j - 2][0] == "k":
+                    back_k(j - 2)
+                if units[j][0] == "k":
+                    multiply_k(j)
+                else:
+                    multiply_v(j, (0, 1))

@@ -10,6 +10,7 @@ U8 = mybir.dt.uint8
 FP8 = mybir.dt.float8_e4m3fn
 FP8X4 = mybir.dt.float8_e4m3fn_x4
 ALU = mybir.AluOpType
+ACT = mybir.ActivationFunctionType
 
 NB, S, DIM, H, HD = 4, 128, 2048, 16, 128
 P = 128
@@ -17,29 +18,48 @@ G = DIM // 512
 TOK = NB * S
 FLOPS = 2 * TOK * DIM * 2 * H * HD
 
+UNITS = (("s", 0), ("k", 0), ("k", 1), ("v", 1), ("k", 2), ("v", 2), ("k", 3), ("v", 3), ("k", 4), ("v", 4), ("k", 5), ("v", 5), ("k", 6), ("v", 6), ("k", 7), ("v", 7))
+ORDERED = (4, 6, 8, 10, 12, 14)
+ORDER_AHEAD = 2
+PIECES = (2, 1, 1, 1, 1, 1, 1, 1, 1, 1, 1, 1, 1, 1, 1)
+LOOKAHEAD = 5
+FIRST_LOADS = (0, "x", 3, 1, 2, 4)
+BV = "dma"
+BV_AT = {}
+SCALE_OUT = "vector"
+CHUNK_FIRST = False
+BACK = 2
+BACK_FIRST = False
+BUFS = {"raw": 5, "vby": 4, "vbf": 4, "prm": 3, "grp": 3, "cod": 3, "rot": 4, "fins": 6, "tp": 4, "acc": 2, "ob": 2}
+VEC_OUT = ()
+LATE_CONST = False
+BV_SLOT = 1
+XVEC = ()
+VEC_BANKS = {}
+LAST_TP = False
+LAST_SPLIT = False
+LAST_ORDER = "h0 back h1"
+WHOLE = 99
+
 
 def tile_attention_pb_kernel(tc, key_value, wk, bk, wv_bytes, wv_scale, bv, cos, sin, out_0, out_1):
     nc = tc.nc
     with ExitStack() as ctx:
         const = ctx.enter_context(tc.tile_pool(name="const", bufs=1))
-        raw = ctx.enter_context(tc.tile_pool(name="raw", bufs=5))
-        vby = ctx.enter_context(tc.tile_pool(name="vby", bufs=4))
-        vbf = ctx.enter_context(tc.tile_pool(name="vbf", bufs=4))
-        prm = ctx.enter_context(tc.tile_pool(name="prm", bufs=3))
-        grp = ctx.enter_context(tc.tile_pool(name="grp", bufs=3))
-        cod = ctx.enter_context(tc.tile_pool(name="cod", bufs=3))
-        rot = ctx.enter_context(tc.tile_pool(name="rot", bufs=4))
-        fins = ctx.enter_context(tc.tile_pool(name="fins", bufs=6))
+        raw = ctx.enter_context(tc.tile_pool(name="raw", bufs=BUFS["raw"]))
+        vby = ctx.enter_context(tc.tile_pool(name="vby", bufs=BUFS["vby"]))
+        vbf = ctx.enter_context(tc.tile_pool(name="vbf", bufs=BUFS["vbf"]))
+        prm = ctx.enter_context(tc.tile_pool(name="prm", bufs=BUFS["prm"]))
+        grp = ctx.enter_context(tc.tile_pool(name="grp", bufs=BUFS["grp"]))
+        cod = ctx.enter_context(tc.tile_pool(name="cod", bufs=BUFS["cod"]))
+        rot = ctx.enter_context(tc.tile_pool(name="rot", bufs=BUFS["rot"]))
+        fins = ctx.enter_context(tc.tile_pool(name="fins", bufs=BUFS["fins"]))
         psum = ctx.enter_context(tc.psum_pool(name="psum", bufs=2))
         ctx.enter_context(tc.manual_schedule())
 
-        units = [("v", 0), ("k", 0)]
-        for i in range(1, 8):
-            units.append(("k", i))
-            units.append(("v", i))
+        units = UNITS
         n_units = len(units)
-        LOOKAHEAD = 5
-        FIRST_ORDERED = 4
+        TPB, ACB, OBB = BUFS["tp"], BUFS["acc"], BUFS["ob"]
 
         s_raw = const.tile([P, P], F32, name="s_raw")
         nc.gpsimd.memset(s_raw[:], 0.0)
@@ -52,6 +72,7 @@ def tile_attention_pb_kernel(tc, key_value, wk, bk, wv_bytes, wv_scale, bv, cos,
         nc.sync.dma_start(out=cs_raw[:, 0, :], in_=cos.rearrange("a b s d -> (a b s) d"))
         nc.sync.dma_start(out=cs_raw[:, 1, :], in_=sin.rearrange("a b s d -> (a b s) d"))
         nc.sync.dma_start(out=b_raw[0:H, :], in_=bk.rearrange("(h d) -> h d", d=HD))
+        nc.sync.dma_start(out=b_raw[H : 2 * H, :], in_=bv.rearrange("(h d) -> h d", d=HD))
 
         scale_b = const.tile([P, DIM], F32, name="scale_b")
         bv_b = const.tile([P, H * HD], BF16, name="bv_b")
@@ -59,6 +80,7 @@ def tile_attention_pb_kernel(tc, key_value, wk, bk, wv_bytes, wv_scale, bv, cos,
         src = {}
         byt = {}
         rawk = {}
+        xr = []
 
         def load(idx):
             kind, i = units[idx]
@@ -72,39 +94,55 @@ def tile_attention_pb_kernel(tc, key_value, wk, bk, wv_bytes, wv_scale, bv, cos,
                 nc.sync.dma_start(out=t[:], in_=wv_bytes[rows, :].rearrange("(r p) k -> p r k", p=P))
                 byt[idx] = t
 
-        load(0)
-        xr = []
-        for j in range(2):
-            xr_t = raw.tile([P, 2, DIM], BF16, tag="raw", name="xr%d" % j)
-            xr.append(xr_t)
-        for b in range(NB):
-            nc.sync.dma_start(out=xr[b // 2][:, b % 2, :], in_=key_value[b])
-        load(3)
-        load(1)
-        load(2)
-        nc.sync.dma_start(out=bv_b[:], in_=bv.partition_broadcast(P))
-        load(4)
+        loaded = []
+        for what in FIRST_LOADS:
+            if what == "x":
+                for j in range(2):
+                    xr_t = raw.tile([P, 2, DIM], BF16, tag="raw", name="xr%d" % j)
+                    xr.append(xr_t)
+                for b in range(NB):
+                    nc.sync.dma_start(out=xr[b // 2][:, b % 2, :], in_=key_value[b])
+            elif what == "bv":
+                nc.sync.dma_start(out=bv_b[:], in_=bv.partition_broadcast(P))
+            else:
+                load(what)
+                loaded.append(what)
+
+        def load_next():
+            for idx in range(n_units):
+                if idx not in loaded:
+                    load(idx)
+                    loaded.append(idx)
+                    return
 
         perm = const.tile([P, P], F32, name="perm")
-        nc.vector.tensor_copy(out=perm[:, 0:64], in_=ident[:, 64:128])
-        nc.vector.tensor_copy(out=perm[:, 64:128], in_=ident[:, 0:64])
         csf = const.tile([P, 2, P], F32, name="csf")
-        nc.vector.tensor_copy(out=csf[:, 0, :], in_=cs_raw[:, 0, :])
-        nc.vector.tensor_copy(out=csf[:, 1, 0:64], in_=cs_raw[:, 1, 64:128])
-        nc.vector.tensor_scalar(out=csf[:, 1, 64:128], in0=cs_raw[:, 1, 0:64], scalar1=-1.0, scalar2=None, op0=ALU.mult)
         b_f = const.tile([P, P], F32, name="b_f")
-        nc.vector.tensor_copy(out=b_f[:], in_=b_raw[:])
+
+        def constants():
+            nc.vector.tensor_copy(out=perm[:, 0:64], in_=ident[:, 64:128])
+            nc.vector.tensor_copy(out=perm[:, 64:128], in_=ident[:, 0:64])
+            nc.vector.tensor_copy(out=csf[:, 0, :], in_=cs_raw[:, 0, :])
+            nc.vector.tensor_copy(out=csf[:, 1, 0:64], in_=cs_raw[:, 1, 64:128])
+            nc.vector.tensor_scalar(out=csf[:, 1, 64:128], in0=cs_raw[:, 1, 0:64], scalar1=-1.0, scalar2=None, op0=ALU.mult)
+            nc.vector.tensor_copy(out=b_f[:], in_=b_raw[:])
+
+        if not LATE_CONST:
+            constants()
 
         scol = const.tile([P, 16], F32, name="scol")
-        tp0 = psum.tile([P, NB, S], F32, tag="tp", bufs=4, name="tp0")
+        tp0 = psum.tile([P, NB, S], F32, tag="tp", bufs=TPB, name="tp0")
         nc.tensor.transpose(tp0[:, 0, :], s_raw[:], ident[:])
         nc.scalar.copy(out=scol[:], in_=tp0[:, 0, 0:16])
         for q in range(4):
-            tpq = psum.tile([P, 4, P], F32, tag="tp", bufs=4, name="tpq")
+            tpq = psum.tile([P, 4, P], F32, tag="tp", bufs=TPB, name="tpq")
             for mm in range(4):
                 m = 4 * q + mm
                 nc.tensor.transpose(tpq[:, mm, :], scol[:, m : m + 1].to_broadcast([P, P]), ident[:])
-            nc.vector.tensor_copy(out=scale_b[:, 512 * q : 512 * (q + 1)], in_=tpq[:].rearrange("p m r -> p (m r)"))
+            if SCALE_OUT == "vector" or (SCALE_OUT == "both" and q % 2 == 1):
+                nc.vector.tensor_copy(out=scale_b[:, 512 * q : 512 * (q + 1)], in_=tpq[:].rearrange("p m r -> p (m r)"))
+            else:
+                nc.scalar.copy(out=scale_b[:, 512 * q : 512 * (q + 1)], in_=tpq[:].rearrange("p m r -> p (m r)"))
 
         x_codes = const.tile([P, G, TOK], U32, name="x_codes", align_bytes=64)
         x_scales = const.tile([P, G, TOK], U8, name="x_scales", align_bytes=64)
@@ -112,47 +150,56 @@ def tile_attention_pb_kernel(tc, key_value, wk, bk, wv_bytes, wv_scale, bv, cos,
         codes = {}
         rots = {}
         groups = {}
+        ordered = {}
 
-        def product(idx, r):
+        def product(idx, r, chunks=1):
             if r == 0:
                 t = vbf.tile([P, 2, DIM], BF16, tag="vbf", name="wvb%d" % idx)
                 src[idx] = t
-            nc.vector.tensor_tensor(out=src[idx][:, r, :], in0=byt[idx][:, r, :].bitcast(FP8), in1=scale_b[:], op=ALU.mult)
+            w = DIM // chunks
+            for c in range(chunks):
+                cols = slice(c * w, (c + 1) * w)
+                nc.vector.tensor_tensor(out=src[idx][:, r, cols], in0=byt[idx][:, r, cols].bitcast(FP8), in1=scale_b[:, cols], op=ALU.mult)
 
         pieces = []
         for idx in range(n_units):
-            if units[idx][0] == "v":
+            if units[idx][0] != "k":
                 pieces.append((idx, 0))
                 pieces.append((idx, 1))
 
-        def next_products(count):
+        def next_products(count, chunks=1):
             for c in range(count):
                 if len(pieces) > 0:
                     idx, r = pieces.pop(0)
-                    product(idx, r)
+                    product(idx, r, chunks if c == 0 else 1)
 
         def permute(idx):
             t = prm.tile([P, 2, G, 2, P], F32, tag="prm", name="wkp%d" % idx)
-            src[idx] = t
+            ordered[idx] = t
+            rows = rawk[idx] if units[idx][0] == "k" else src[idx]
             for r in range(2):
-                nc.scalar.copy(out=t[:, r, :, :, :], in_=rawk[idx][:, r, :].bitcast(F32).rearrange("p (g j u) -> p g u j", g=G, u=2))
+                nc.scalar.copy(out=t[:, r, :, :, :], in_=rows[:, r, :].bitcast(F32).rearrange("p (g j u) -> p g u j", g=G, u=2))
 
         def turn(idx):
             wg = grp.tile([P, G, 256, 4], BF16, tag="grp", name="wg%d" % idx, align_bytes=64)
             groups[idx] = wg
             for r in range(2):
                 for gp in range(2):
-                    tp = psum.tile([P, 2, 2, P], F32, tag="tp", bufs=4, name="tpw")
+                    tp = psum.tile([P, 2, 2, P], F32, tag="tp", bufs=TPB, name="tpw")
                     for gg in range(2):
                         g = 2 * gp + gg
                         for u in range(2):
-                            if units[idx][0] == "k" and idx >= FIRST_ORDERED:
-                                nc.tensor.transpose(tp[:, gg, u, :], src[idx][:, r, g, u, :], ident[:])
+                            if idx in ORDERED:
+                                nc.tensor.transpose(tp[:, gg, u, :], ordered[idx][:, r, g, u, :], ident[:])
                             else:
                                 rows = rawk[idx] if units[idx][0] == "k" else src[idx]
                                 words = rows[:, r, :].bitcast(F32)
                                 nc.tensor.transpose(tp[:, gg, u, :], words[:, 256 * g + u : 256 * (g + 1) : 2], ident[:])
-                    nc.scalar.copy(out=wg[:, 2 * gp : 2 * gp + 2, r * P : (r + 1) * P, :].bitcast(F32), in_=tp[:].rearrange("p g u c -> p g c u"))
+                    dst = wg[:, 2 * gp : 2 * gp + 2, r * P : (r + 1) * P, :].bitcast(F32)
+                    if (idx in VEC_OUT and gp == 1) or (r, gp) in VEC_BANKS.get(idx, ()):
+                        nc.vector.tensor_copy(out=dst, in_=tp[:].rearrange("p g u c -> p g c u"))
+                    else:
+                        nc.scalar.copy(out=dst, in_=tp[:].rearrange("p g u c -> p g c u"))
 
         def quantise(idx):
             wc = cod.tile([P, G * 256], U32, tag="wc", name="wc%d" % idx, align_bytes=64)
@@ -160,13 +207,13 @@ def tile_attention_pb_kernel(tc, key_value, wk, bk, wv_bytes, wv_scale, bv, cos,
             nc.vector.quantize_mx(out=wc[:].bitcast(FP8X4), scales=ws[:], in_=groups[idx][:].rearrange("p g c t -> p (g c t)"))
             codes[idx] = (wc, ws)
 
-        def multiply_k(idx):
-            i = units[idx][1]
+        def multiply_w(idx):
+            kind, i = units[idx]
             wc, ws = codes[idx]
             pair = []
             for r in range(2):
                 h = 2 * i + r
-                acc = psum.tile([P, TOK], F32, tag="acc", bufs=2, name="acck")
+                acc = psum.tile([P, TOK], F32, tag="acc", bufs=ACB, name="acck")
                 for g in range(G):
                     cols = slice(g * 256 + r * P, g * 256 + (r + 1) * P)
                     nc.tensor.matmul_mx(
@@ -178,37 +225,71 @@ def tile_attention_pb_kernel(tc, key_value, wk, bk, wv_bytes, wv_scale, bv, cos,
                         start=(g == 0),
                         stop=(g == G - 1),
                     )
-                rab = rot.tile([P, 2, TOK], F32, tag="rab", name="rab%d" % h)
-                nc.vector.scalar_tensor_tensor(
-                    out=rab[:],
-                    in0=acc[:].unsqueeze(1).to_broadcast([P, 2, TOK]),
-                    scalar=bias_t[:, h : h + 1],
-                    in1=cs2[:].rearrange("p c b s -> p c (b s)"),
-                    op0=ALU.add,
-                    op1=ALU.mult,
-                )
+                if kind == "k":
+                    rab = rot.tile([P, 2, TOK], F32, tag="rab", name="rab%d" % h)
+                    nc.vector.scalar_tensor_tensor(
+                        out=rab[:],
+                        in0=acc[:].unsqueeze(1).to_broadcast([P, 2, TOK]),
+                        scalar=bias_t[:, h : h + 1],
+                        in1=cs2[:].rearrange("p c b s -> p c (b s)"),
+                        op0=ALU.add,
+                        op1=ALU.mult,
+                    )
+                else:
+                    rab = rot.tile([P, TOK], F32, tag="rab", name="vb%d" % h)
+                    nc.scalar.activation(out=rab[:], in_=acc[:], func=ACT.Identity, bias=bias_t[:, H + h : H + h + 1], scale=1.0)
                 pair.append(rab)
             rots[idx] = pair
 
-        def back_k(idx):
-            i = units[idx][1]
+        pending = []
+
+        def back_upto(last):
+            for idx in list(pending):
+                if idx <= last:
+                    pending.remove(idx)
+                    back(idx)
+
+        def back(idx):
+            kind, i = units[idx]
             for r in range(2):
                 h = 2 * i + r
                 rab = rots[idx][r]
-                ob = psum.tile([P, NB, HD], F32, tag="ob", bufs=2, name="ob")
+                ob = psum.tile([P, NB, HD], F32, tag="ob", bufs=OBB, name="ob")
                 for b in range(NB):
                     cols = slice(b * S, (b + 1) * S)
-                    nc.tensor.matmul(ob[:, b, :], lhsT=rab[:, 0, cols], rhs=ident[:], is_transpose=True, start=True, stop=False)
-                    nc.tensor.matmul(ob[:, b, :], lhsT=rab[:, 1, cols], rhs=perm[:], is_transpose=True, start=False, stop=True)
+                    if kind == "k":
+                        nc.tensor.matmul(ob[:, b, :], lhsT=rab[:, 0, cols], rhs=ident[:], is_transpose=True, start=True, stop=False)
+                        nc.tensor.matmul(ob[:, b, :], lhsT=rab[:, 1, cols], rhs=perm[:], is_transpose=True, start=False, stop=True)
+                    else:
+                        nc.tensor.transpose(ob[:, b, :], rab[:, cols], ident[:])
                 fin = fins.tile([P, NB, HD], F32, tag="fin", name="fink")
                 nc.scalar.copy(out=fin[:], in_=ob[:])
-                nc.sync.dma_start(out=out_0[:, h, :, :].rearrange("b s d -> s b d"), in_=fin[:])
+                dst = out_0 if kind == "k" else out_1
+                nc.sync.dma_start(out=dst[:, h, :, :].rearrange("b s d -> s b d"), in_=fin[:])
 
-        def multiply_v(idx, halves):
+        def multiply_v1(idx, b, tag, nbufs):
+            i = units[idx][1]
+            wc, ws = codes[idx]
+            acc = psum.tile([P, 256], F32, tag=tag, bufs=nbufs, name="accb")
+            for g in range(G):
+                nc.tensor.matmul_mx(
+                    out=acc[:],
+                    lhsT=x_codes[:, g, b * S : (b + 1) * S].bitcast(FP8X4),
+                    lhsT_scale=x_scales[:, g, b * S : (b + 1) * S],
+                    rhs=wc[:, g * 256 : (g + 1) * 256].bitcast(FP8X4),
+                    rhs_scale=ws[:, g * 256 : (g + 1) * 256],
+                    start=(g == 0),
+                    stop=(g == G - 1),
+                )
+            fin = fins.tile([P, 256], F32, tag="fin", name="finb")
+            nc.vector.tensor_tensor(out=fin[:], in0=acc[:], in1=bv_b[:, 256 * i : 256 * (i + 1)], op=ALU.add)
+            nc.sync.dma_start(out=out_1[b, 2 * i : 2 * i + 2, :, :].rearrange("h s d -> s h d"), in_=fin[:].rearrange("p (h d) -> p h d", d=HD))
+
+        def multiply_v(idx, halves, tag="acc", nbufs=None):
             i = units[idx][1]
             wc, ws = codes[idx]
             for bp in halves:
-                acc = psum.tile([P, 2, 256], F32, tag="acc", bufs=2, name="accv")
+                acc = psum.tile([P, 2, 256], F32, tag=tag, bufs=nbufs or ACB, name="accv")
                 for bb in range(2):
                     b = 2 * bp + bb
                     for g in range(G):
@@ -235,7 +316,16 @@ def tile_attention_pb_kernel(tc, key_value, wk, bk, wv_bytes, wv_scale, bv, cos,
                         in_=fin[:, bb, :].rearrange("p (h d) -> p h d", d=HD),
                     )
 
-        next_products(2)
+        def spread_bv(q):
+            tpb = psum.tile([P, 4, P], F32, tag="tp", bufs=TPB, name="tpb")
+            for mm in range(4):
+                h = 4 * q + mm
+                nc.tensor.transpose(tpb[:, mm, :], bias_t[:, H + h : H + h + 1].to_broadcast([P, P]), ident[:])
+            nc.scalar.copy(out=bv_b[:, 512 * q : 512 * (q + 1)], in_=tpb[:].rearrange("p m r -> p (m r)"))
+
+        next_products(PIECES[0], 4 if CHUNK_FIRST else 1)
+        if LATE_CONST:
+            constants()
 
         xg = []
         for gp in range(2):
@@ -244,13 +334,16 @@ def tile_attention_pb_kernel(tc, key_value, wk, bk, wv_bytes, wv_scale, bv, cos,
         for b in range(NB):
             words = xr[b // 2][:, b % 2, :].bitcast(F32)
             for gp in range(2):
-                tp = psum.tile([P, 2, 2, P], F32, tag="tp", bufs=4, name="tpx")
+                tp = psum.tile([P, 2, 2, P], F32, tag="tp", bufs=TPB, name="tpx")
                 for gg in range(2):
                     g = 2 * gp + gg
                     for u in range(2):
                         nc.tensor.transpose(tp[:, gg, u, :], words[:, 256 * g + u : 256 * (g + 1) : 2], ident[:])
                 dst = xg[gp][:, :, b * P : (b + 1) * P, :].bitcast(F32)
-                nc.scalar.copy(out=dst, in_=tp[:].rearrange("p g u c -> p g c u"))
+                if (b, gp) in XVEC:
+                    nc.vector.tensor_copy(out=dst, in_=tp[:].rearrange("p g u c -> p g c u"))
+                else:
+                    nc.scalar.copy(out=dst, in_=tp[:].rearrange("p g u c -> p g c u"))
         for gp in range(2):
             nc.vector.quantize_mx(
                 out=x_codes[:, 2 * gp : 2 * gp + 2, :].rearrange("p g c -> p (g c)").bitcast(FP8X4),
@@ -262,34 +355,49 @@ def tile_attention_pb_kernel(tc, key_value, wk, bk, wv_bytes, wv_scale, bv, cos,
         quantise(0)
 
         cst = const.tile([P, 3, P], F32, name="cst")
-        tpc = psum.tile([P, 4, P], F32, tag="tp", bufs=4, name="tpc")
+        tpc = psum.tile([P, 4, P], F32, tag="tp", bufs=TPB, name="tpc")
         nc.tensor.transpose(tpc[:, 0, :], csf[:, 0, :], ident[:])
         nc.tensor.transpose(tpc[:, 1, :], csf[:, 1, :], ident[:])
         nc.tensor.transpose(tpc[:, 2, :], b_f[:], ident[:])
         nc.scalar.copy(out=cst[:], in_=tpc[:, 0:3, :])
         bias_t = cst[:, 2, :]
         cs2 = const.tile([P, 2, NB, S], F32, name="cs2")
+        if BV == "pe" and -1 in BV_AT:
+            spread_bv(BV_AT[-1])
 
         for j in range(n_units):
-            if j + LOOKAHEAD < n_units:
-                load(j + LOOKAHEAD)
-            next_products(1)
+            if len(loaded) < n_units:
+                load_next()
+            if BV_SLOT == j:
+                nc.sync.dma_start(out=bv_b[:], in_=bv.partition_broadcast(P))
+            next_products(PIECES[j + 1] if j + 1 < len(PIECES) else 0)
+            if BACK_FIRST and j < n_units - 1:
+                back_upto(j - BACK)
             if j + 1 < n_units:
                 turn(j + 1)
             if j == 0:
                 nc.scalar.copy(out=cs2[:], in_=cst[:, 0:2, :].unsqueeze(2).to_broadcast([P, 2, NB, S]))
-            if j + 2 < n_units and units[j + 2][0] == "k" and j + 2 >= FIRST_ORDERED:
-                permute(j + 2)
+            if BV == "pe" and j in BV_AT:
+                spread_bv(BV_AT[j])
+            if j + ORDER_AHEAD in ORDERED:
+                permute(j + ORDER_AHEAD)
             if j + 1 < n_units:
                 quantise(j + 1)
             if j == n_units - 1:
-                multiply_v(j, (0,))
-                back_k(j - 1)
-                multiply_v(j, (1,))
+                tg, nb = ("tp", TPB) if LAST_TP else ("acc", ACB)
+                for step in LAST_ORDER.split():
+                    if step == "back":
+                        back_upto(j)
+                    elif LAST_SPLIT:
+                        multiply_v1(j, 2 * int(step[1]), tg, nb)
+                        multiply_v1(j, 2 * int(step[1]) + 1, tg, nb)
+                    else:
+                        multiply_v(j, (int(step[1]),), tg, nb)
             else:
-                if j >= 2 and units[j - 2][0] == "k":
-                    back_k(j - 2)
-                if units[j][0] == "k":
-                    multiply_k(j)
-                else:
+                if not BACK_FIRST:
+                    back_upto(j - BACK)
+                if units[j][0] == "v":
                     multiply_v(j, (0, 1))
+                else:
+                    multiply_w(j)
+                    pending.append(j)

@@ -39,6 +39,10 @@ VEC_BANKS = {}
 LAST_TP = False
 LAST_SPLIT = False
 LAST_ORDER = "h0 back h1"
+WARM_START = 6
+WARM_SCALE = 3
+WARM_X = 1
+WARM_UNITS = {0: 1, 1: 1, 2: 1}
 WHOLE = 99
 
 
@@ -61,6 +65,17 @@ def tile_attention_pb_kernel(tc, key_value, wk, bk, wv_bytes, wv_scale, bv, cos,
         n_units = len(units)
         TPB, ACB, OBB = BUFS["tp"], BUFS["acc"], BUFS["ob"]
 
+        warm_in = const.tile([P, TOK], BF16, name="warm_in")
+        if WARM_START + WARM_SCALE + WARM_X + len(WARM_UNITS) > 0:
+            nc.vector.memset(warm_in[:], 0.0)
+
+        def warm(count):
+            if count > 0:
+                wps = psum.tile([P, TOK], F32, tag="acc", bufs=BUFS["acc"], name="wps")
+                for c in range(count):
+                    nc.tensor.matmul(wps[:], lhsT=warm_in[:, 0:P], rhs=warm_in[:], start=True, stop=True)
+
+        warm(WARM_START)
         s_raw = const.tile([P, P], F32, name="s_raw")
         nc.gpsimd.memset(s_raw[:], 0.0)
         b_raw = const.tile([P, P], BF16, name="b_raw")
@@ -144,6 +159,7 @@ def tile_attention_pb_kernel(tc, key_value, wk, bk, wv_bytes, wv_scale, bv, cos,
             else:
                 nc.scalar.copy(out=scale_b[:, 512 * q : 512 * (q + 1)], in_=tpq[:].rearrange("p m r -> p (m r)"))
 
+        warm(WARM_SCALE)
         x_codes = const.tile([P, G, TOK], U32, name="x_codes", align_bytes=64)
         x_scales = const.tile([P, G, TOK], U8, name="x_scales", align_bytes=64)
 
@@ -200,6 +216,7 @@ def tile_attention_pb_kernel(tc, key_value, wk, bk, wv_bytes, wv_scale, bv, cos,
                         nc.vector.tensor_copy(out=dst, in_=tp[:].rearrange("p g u c -> p g c u"))
                     else:
                         nc.scalar.copy(out=dst, in_=tp[:].rearrange("p g u c -> p g c u"))
+                warm(WARM_UNITS.get(idx, 0))
 
         def quantise(idx):
             wc = cod.tile([P, G * 256], U32, tag="wc", name="wc%d" % idx, align_bytes=64)
@@ -344,6 +361,7 @@ def tile_attention_pb_kernel(tc, key_value, wk, bk, wv_bytes, wv_scale, bv, cos,
                     nc.vector.tensor_copy(out=dst, in_=tp[:].rearrange("p g u c -> p g c u"))
                 else:
                     nc.scalar.copy(out=dst, in_=tp[:].rearrange("p g u c -> p g c u"))
+            warm(WARM_X)
         for gp in range(2):
             nc.vector.quantize_mx(
                 out=x_codes[:, 2 * gp : 2 * gp + 2, :].rearrange("p g c -> p (g c)").bitcast(FP8X4),

@@ -43,6 +43,7 @@ WARM_START = 6
 WARM_SCALE = 3
 WARM_X = 1
 WARM_UNITS = {0: 1, 1: 1, 2: 1}
+WARM_BANKS = {3: ((1, 0),), 5: ((1, 0),), 7: ((1, 0),), 9: ((1, 0),), 11: ((1, 0),), 13: ((1, 0),), 15: ((1, 0),)}
 WHOLE = 99
 
 
@@ -66,7 +67,7 @@ def tile_attention_pb_kernel(tc, key_value, wk, bk, wv_bytes, wv_scale, bv, cos,
         TPB, ACB, OBB = BUFS["tp"], BUFS["acc"], BUFS["ob"]
 
         warm_in = const.tile([P, TOK], BF16, name="warm_in")
-        if WARM_START + WARM_SCALE + WARM_X + len(WARM_UNITS) > 0:
+        if WARM_START + WARM_SCALE + WARM_X + len(WARM_UNITS) + len(WARM_BANKS) > 0:
             nc.vector.memset(warm_in[:], 0.0)
 
         def warm(count):
@@ -202,6 +203,8 @@ def tile_attention_pb_kernel(tc, key_value, wk, bk, wv_bytes, wv_scale, bv, cos,
             for r in range(2):
                 for gp in range(2):
                     tp = psum.tile([P, 2, 2, P], F32, tag="tp", bufs=TPB, name="tpw")
+                    if (r, gp) in WARM_BANKS.get(idx, ()):
+                        nc.tensor.matmul(tp[:].rearrange("p g u c -> p (g u c)"), lhsT=warm_in[:, 0:P], rhs=warm_in[:], start=True, stop=True)
                     for gg in range(2):
                         g = 2 * gp + gg
                         for u in range(2):

@@ -36,12 +36,13 @@ LATE_CONST = False
 BV_SLOT = 1
 XVEC = ()
 VEC_BANKS = {}
-LAST_TP = False
-LAST_SPLIT = False
+LAST_TP = True
+LAST_SPLIT = True
 LAST_ORDER = "h0 back h1"
 WARM_START = 6
 WARM_SCALE = 3
 WARM_X = 1
+WARM_XB = (0, 1, 2, 3)
 WARM_UNITS = {0: 1, 1: 1, 2: 1}
 WARM_BANKS = {3: ((1, 0),), 5: ((1, 0),), 7: ((1, 0),), 9: ((1, 0),), 11: ((1, 0),), 13: ((1, 0),), 15: ((1, 0),)}
 WHOLE = 99
@@ -90,7 +91,8 @@ def tile_attention_pb_kernel(tc, key_value, wk, bk, wv_bytes, wv_scale, bv, cos,
         nc.sync.dma_start(out=b_raw[0:H, :], in_=bk.rearrange("(h d) -> h d", d=HD))
         nc.sync.dma_start(out=b_raw[H : 2 * H, :], in_=bv.rearrange("(h d) -> h d", d=HD))
 
-        scale_b = const.tile([P, DIM], F32, name="scale_b")
+        scale_2 = const.tile([P, 2, DIM], F32, name="scale_2")
+        scale_b = scale_2[:, 0, :]
         bv_b = const.tile([P, H * HD], BF16, name="bv_b")
 
         src = {}
@@ -159,6 +161,8 @@ def tile_attention_pb_kernel(tc, key_value, wk, bk, wv_bytes, wv_scale, bv, cos,
                 nc.vector.tensor_copy(out=scale_b[:, 512 * q : 512 * (q + 1)], in_=tpq[:].rearrange("p m r -> p (m r)"))
             else:
                 nc.scalar.copy(out=scale_b[:, 512 * q : 512 * (q + 1)], in_=tpq[:].rearrange("p m r -> p (m r)"))
+            if WHOLE < 99:
+                nc.scalar.copy(out=scale_2[:, 1, 512 * q : 512 * (q + 1)], in_=tpq[:].rearrange("p m r -> p (m r)"))
 
         warm(WARM_SCALE)
         x_codes = const.tile([P, G, TOK], U32, name="x_codes", align_bytes=64)
@@ -184,11 +188,25 @@ def tile_attention_pb_kernel(tc, key_value, wk, bk, wv_bytes, wv_scale, bv, cos,
                 pieces.append((idx, 0))
                 pieces.append((idx, 1))
 
+        def product2(idx):
+            t = vbf.tile([P, 2, DIM], BF16, tag="vbf", name="wvb%d" % idx)
+            src[idx] = t
+            nc.vector.tensor_tensor(
+                out=t[:].rearrange("p r k -> p (r k)"),
+                in0=byt[idx][:].rearrange("p r k -> p (r k)").bitcast(FP8),
+                in1=scale_2[:].rearrange("p r k -> p (r k)"),
+                op=ALU.mult,
+            )
+
         def next_products(count, chunks=1):
             for c in range(count):
                 if len(pieces) > 0:
                     idx, r = pieces.pop(0)
-                    product(idx, r, chunks if c == 0 else 1)
+                    if 16 - len(pieces) - 1 >= WHOLE:
+                        if r == 0:
+                            product2(idx)
+                    else:
+                        product(idx, r, chunks if c == 0 else 1)
 
         def permute(idx):
             t = prm.tile([P, 2, G, 2, P], F32, tag="prm", name="wkp%d" % idx)
@@ -364,7 +382,7 @@ def tile_attention_pb_kernel(tc, key_value, wk, bk, wv_bytes, wv_scale, bv, cos,
                     nc.vector.tensor_copy(out=dst, in_=tp[:].rearrange("p g u c -> p g c u"))
                 else:
                     nc.scalar.copy(out=dst, in_=tp[:].rearrange("p g u c -> p g c u"))
-            warm(WARM_X)
+            warm(WARM_X if b in WARM_XB else 0)
         for gp in range(2):
             nc.vector.quantize_mx(
                 out=x_codes[:, 2 * gp : 2 * gp + 2, :].rearrange("p g c -> p (g c)").bitcast(FP8X4),

@@ -16,68 +16,47 @@ NB, S, DIM, H, HD = 4, 128, 2048, 16, 128
 P = 128
 G = DIM // 512
 TOK = NB * S
+ROWS = 2 * HD
 FLOPS = 2 * TOK * DIM * 2 * H * HD
 
-UNITS = (("s", 0), ("k", 0), ("k", 1), ("v", 1), ("k", 2), ("v", 2), ("k", 3), ("v", 3), ("k", 4), ("v", 4), ("k", 5), ("v", 5), ("k", 6), ("v", 6), ("k", 7), ("v", 7))
-ORDERED = (4, 6, 8, 10, 12, 14)
-ORDER_AHEAD = 2
-PIECES = (2, 1, 1, 1, 1, 1, 1, 1, 1, 1, 1, 1, 1, 1, 1)
-LOOKAHEAD = 5
-FIRST_LOADS = (0, "x", 3, 1, 2, 4)
-BV = "dma"
-BV_AT = {}
-SCALE_OUT = "vector"
-CHUNK_FIRST = False
-BACK = 2
-BACK_FIRST = False
-BUFS = {"raw": 5, "vby": 4, "vbf": 4, "prm": 3, "grp": 3, "cod": 3, "rot": 4, "fins": 6, "tp": 4, "acc": 2, "ob": 2}
-VEC_OUT = ()
-LATE_CONST = False
-BV_SLOT = 1
-XVEC = ()
-VEC_BANKS = {}
-LAST_TP = True
-LAST_SPLIT = True
-LAST_ORDER = "h0 back h1"
-WARM_START = 6
-WARM_SCALE = 3
-WARM_X = 1
-WARM_XB = (0, 1, 2, 3)
-WARM_UNITS = {0: 1, 1: 1, 2: 1}
-WARM_BANKS = {3: ((1, 0),), 5: ((1, 0),), 7: ((1, 0),), 9: ((1, 0),), 11: ((1, 0),), 13: ((1, 0),), 15: ((1, 0),)}
-WHOLE = 99
+UNITS = (
+    ("s", 0), ("k", 0), ("k", 1), ("v", 1), ("k", 2), ("v", 2), ("k", 3), ("v", 3),
+    ("k", 4), ("v", 4), ("k", 5), ("v", 5), ("k", 6), ("v", 6), ("k", 7), ("v", 7),
+)
+N_UNITS = len(UNITS)
+FIRST_ORDERED = 4
+FIRST_LOADS = (3, 1, 2, 4)
+TP_BANKS, ACC_BANKS, OB_BANKS = 4, 2, 2
 
 
 def tile_attention_pb_kernel(tc, key_value, wk, bk, wv_bytes, wv_scale, bv, cos, sin, out_0, out_1):
     nc = tc.nc
     with ExitStack() as ctx:
         const = ctx.enter_context(tc.tile_pool(name="const", bufs=1))
-        raw = ctx.enter_context(tc.tile_pool(name="raw", bufs=BUFS["raw"]))
-        vby = ctx.enter_context(tc.tile_pool(name="vby", bufs=BUFS["vby"]))
-        vbf = ctx.enter_context(tc.tile_pool(name="vbf", bufs=BUFS["vbf"]))
-        prm = ctx.enter_context(tc.tile_pool(name="prm", bufs=BUFS["prm"]))
-        grp = ctx.enter_context(tc.tile_pool(name="grp", bufs=BUFS["grp"]))
-        cod = ctx.enter_context(tc.tile_pool(name="cod", bufs=BUFS["cod"]))
-        rot = ctx.enter_context(tc.tile_pool(name="rot", bufs=BUFS["rot"]))
-        fins = ctx.enter_context(tc.tile_pool(name="fins", bufs=BUFS["fins"]))
+        raw = ctx.enter_context(tc.tile_pool(name="raw", bufs=5))
+        vby = ctx.enter_context(tc.tile_pool(name="vby", bufs=4))
+        vbf = ctx.enter_context(tc.tile_pool(name="vbf", bufs=4))
+        prm = ctx.enter_context(tc.tile_pool(name="prm", bufs=3))
+        grp = ctx.enter_context(tc.tile_pool(name="grp", bufs=3))
+        cod = ctx.enter_context(tc.tile_pool(name="cod", bufs=3))
+        rot = ctx.enter_context(tc.tile_pool(name="rot", bufs=4))
+        fins = ctx.enter_context(tc.tile_pool(name="fins", bufs=6))
         psum = ctx.enter_context(tc.psum_pool(name="psum", bufs=2))
         ctx.enter_context(tc.manual_schedule())
 
-        units = UNITS
-        n_units = len(units)
-        TPB, ACB, OBB = BUFS["tp"], BUFS["acc"], BUFS["ob"]
+        zeros = const.tile([P, TOK], BF16, name="zeros")
+        nc.vector.memset(zeros[:], 0.0)
 
-        warm_in = const.tile([P, TOK], BF16, name="warm_in")
-        if WARM_START + WARM_SCALE + WARM_X + len(WARM_UNITS) + len(WARM_BANKS) > 0:
-            nc.vector.memset(warm_in[:], 0.0)
+        def keep_clock(bank):
+            nc.tensor.matmul(bank, lhsT=zeros[:, 0:P], rhs=zeros[:], start=True, stop=True)
 
-        def warm(count):
-            if count > 0:
-                wps = psum.tile([P, TOK], F32, tag="acc", bufs=BUFS["acc"], name="wps")
-                for c in range(count):
-                    nc.tensor.matmul(wps[:], lhsT=warm_in[:, 0:P], rhs=warm_in[:], start=True, stop=True)
+        def keep_clock_in_free_bank(count):
+            bank = psum.tile([P, TOK], F32, tag="acc", bufs=ACC_BANKS, name="idle")
+            for c in range(count):
+                keep_clock(bank[:])
 
-        warm(WARM_START)
+        keep_clock_in_free_bank(6)
+
         s_raw = const.tile([P, P], F32, name="s_raw")
         nc.gpsimd.memset(s_raw[:], 0.0)
         b_raw = const.tile([P, P], BF16, name="b_raw")
@@ -91,169 +70,131 @@ def tile_attention_pb_kernel(tc, key_value, wk, bk, wv_bytes, wv_scale, bv, cos,
         nc.sync.dma_start(out=b_raw[0:H, :], in_=bk.rearrange("(h d) -> h d", d=HD))
         nc.sync.dma_start(out=b_raw[H : 2 * H, :], in_=bv.rearrange("(h d) -> h d", d=HD))
 
-        scale_2 = const.tile([P, 2, DIM], F32, name="scale_2")
-        scale_b = scale_2[:, 0, :]
+        scale_b = const.tile([P, DIM], F32, name="scale_b")
         bv_b = const.tile([P, H * HD], BF16, name="bv_b")
 
-        src = {}
-        byt = {}
-        rawk = {}
-        xr = []
+        wk_rows = {}
+        wv_codes_in = {}
+        wv_rows = {}
+        loaded = []
 
         def load(idx):
-            kind, i = units[idx]
-            rows = slice(256 * i, 256 * (i + 1))
+            kind, i = UNITS[idx]
+            rows = slice(ROWS * i, ROWS * (i + 1))
             if kind == "k":
                 t = raw.tile([P, 2, DIM], BF16, tag="raw", name="wkr%d" % i)
                 nc.sync.dma_start(out=t[:], in_=wk[rows, :].rearrange("(r p) k -> p r k", p=P))
-                rawk[idx] = t
+                wk_rows[idx] = t
             else:
                 t = vby.tile([P, 2, DIM], U8, tag="vby", name="wvy%d" % i)
                 nc.sync.dma_start(out=t[:], in_=wv_bytes[rows, :].rearrange("(r p) k -> p r k", p=P))
-                byt[idx] = t
+                wv_codes_in[idx] = t
+            loaded.append(idx)
 
-        loaded = []
-        for what in FIRST_LOADS:
-            if what == "x":
-                for j in range(2):
-                    xr_t = raw.tile([P, 2, DIM], BF16, tag="raw", name="xr%d" % j)
-                    xr.append(xr_t)
-                for b in range(NB):
-                    nc.sync.dma_start(out=xr[b // 2][:, b % 2, :], in_=key_value[b])
-            elif what == "bv":
-                nc.sync.dma_start(out=bv_b[:], in_=bv.partition_broadcast(P))
-            else:
-                load(what)
-                loaded.append(what)
-
-        def load_next():
-            for idx in range(n_units):
-                if idx not in loaded:
-                    load(idx)
-                    loaded.append(idx)
-                    return
+        load(0)
+        x_rows = []
+        for j in range(2):
+            x_t = raw.tile([P, 2, DIM], BF16, tag="raw", name="xr%d" % j)
+            x_rows.append(x_t)
+        for b in range(NB):
+            nc.sync.dma_start(out=x_rows[b // 2][:, b % 2, :], in_=key_value[b])
+        for idx in FIRST_LOADS:
+            load(idx)
 
         perm = const.tile([P, P], F32, name="perm")
         csf = const.tile([P, 2, P], F32, name="csf")
         b_f = const.tile([P, P], F32, name="b_f")
-
-        def constants():
-            nc.vector.tensor_copy(out=perm[:, 0:64], in_=ident[:, 64:128])
-            nc.vector.tensor_copy(out=perm[:, 64:128], in_=ident[:, 0:64])
-            nc.vector.tensor_copy(out=csf[:, 0, :], in_=cs_raw[:, 0, :])
-            nc.vector.tensor_copy(out=csf[:, 1, 0:64], in_=cs_raw[:, 1, 64:128])
-            nc.vector.tensor_scalar(out=csf[:, 1, 64:128], in0=cs_raw[:, 1, 0:64], scalar1=-1.0, scalar2=None, op0=ALU.mult)
-            nc.vector.tensor_copy(out=b_f[:], in_=b_raw[:])
-
-        if not LATE_CONST:
-            constants()
+        nc.vector.tensor_copy(out=perm[:, 0:64], in_=ident[:, 64:128])
+        nc.vector.tensor_copy(out=perm[:, 64:128], in_=ident[:, 0:64])
+        nc.vector.tensor_copy(out=csf[:, 0, :], in_=cs_raw[:, 0, :])
+        nc.vector.tensor_copy(out=csf[:, 1, 0:64], in_=cs_raw[:, 1, 64:128])
+        nc.vector.tensor_scalar(out=csf[:, 1, 64:128], in0=cs_raw[:, 1, 0:64], scalar1=-1.0, scalar2=None, op0=ALU.mult)
+        nc.vector.tensor_copy(out=b_f[:], in_=b_raw[:])
 
         scol = const.tile([P, 16], F32, name="scol")
-        tp0 = psum.tile([P, NB, S], F32, tag="tp", bufs=TPB, name="tp0")
+        tp0 = psum.tile([P, NB, S], F32, tag="tp", bufs=TP_BANKS, name="tp0")
         nc.tensor.transpose(tp0[:, 0, :], s_raw[:], ident[:])
         nc.scalar.copy(out=scol[:], in_=tp0[:, 0, 0:16])
         for q in range(4):
-            tpq = psum.tile([P, 4, P], F32, tag="tp", bufs=TPB, name="tpq")
+            tpq = psum.tile([P, 4, P], F32, tag="tp", bufs=TP_BANKS, name="tpq")
             for mm in range(4):
                 m = 4 * q + mm
                 nc.tensor.transpose(tpq[:, mm, :], scol[:, m : m + 1].to_broadcast([P, P]), ident[:])
-            if SCALE_OUT == "vector" or (SCALE_OUT == "both" and q % 2 == 1):
-                nc.vector.tensor_copy(out=scale_b[:, 512 * q : 512 * (q + 1)], in_=tpq[:].rearrange("p m r -> p (m r)"))
-            else:
-                nc.scalar.copy(out=scale_b[:, 512 * q : 512 * (q + 1)], in_=tpq[:].rearrange("p m r -> p (m r)"))
-            if WHOLE < 99:
-                nc.scalar.copy(out=scale_2[:, 1, 512 * q : 512 * (q + 1)], in_=tpq[:].rearrange("p m r -> p (m r)"))
+            nc.vector.tensor_copy(out=scale_b[:, 512 * q : 512 * (q + 1)], in_=tpq[:].rearrange("p m r -> p (m r)"))
+        keep_clock_in_free_bank(3)
 
-        warm(WARM_SCALE)
         x_codes = const.tile([P, G, TOK], U32, name="x_codes", align_bytes=64)
         x_scales = const.tile([P, G, TOK], U8, name="x_scales", align_bytes=64)
 
-        codes = {}
-        rots = {}
-        groups = {}
         ordered = {}
+        groups = {}
+        codes = {}
+        turned = {}
+        to_turn_back = []
 
-        def product(idx, r, chunks=1):
+        def product(idx, r):
             if r == 0:
                 t = vbf.tile([P, 2, DIM], BF16, tag="vbf", name="wvb%d" % idx)
-                src[idx] = t
-            w = DIM // chunks
-            for c in range(chunks):
-                cols = slice(c * w, (c + 1) * w)
-                nc.vector.tensor_tensor(out=src[idx][:, r, cols], in0=byt[idx][:, r, cols].bitcast(FP8), in1=scale_b[:, cols], op=ALU.mult)
+                wv_rows[idx] = t
+            nc.vector.tensor_tensor(out=wv_rows[idx][:, r, :], in0=wv_codes_in[idx][:, r, :].bitcast(FP8), in1=scale_b[:], op=ALU.mult)
 
-        pieces = []
-        for idx in range(n_units):
-            if units[idx][0] != "k":
-                pieces.append((idx, 0))
-                pieces.append((idx, 1))
+        row_tiles = []
+        for idx in range(N_UNITS):
+            if UNITS[idx][0] != "k":
+                row_tiles.append((idx, 0))
+                row_tiles.append((idx, 1))
 
-        def product2(idx):
-            t = vbf.tile([P, 2, DIM], BF16, tag="vbf", name="wvb%d" % idx)
-            src[idx] = t
-            nc.vector.tensor_tensor(
-                out=t[:].rearrange("p r k -> p (r k)"),
-                in0=byt[idx][:].rearrange("p r k -> p (r k)").bitcast(FP8),
-                in1=scale_2[:].rearrange("p r k -> p (r k)"),
-                op=ALU.mult,
-            )
-
-        def next_products(count, chunks=1):
+        def next_products(count):
             for c in range(count):
-                if len(pieces) > 0:
-                    idx, r = pieces.pop(0)
-                    if 16 - len(pieces) - 1 >= WHOLE:
-                        if r == 0:
-                            product2(idx)
-                    else:
-                        product(idx, r, chunks if c == 0 else 1)
+                if len(row_tiles) > 0:
+                    idx, r = row_tiles.pop(0)
+                    product(idx, r)
 
-        def permute(idx):
+        def contiguous_words(idx):
+            return UNITS[idx][0] == "k" and idx >= FIRST_ORDERED
+
+        def order_words(idx):
             t = prm.tile([P, 2, G, 2, P], F32, tag="prm", name="wkp%d" % idx)
             ordered[idx] = t
-            rows = rawk[idx] if units[idx][0] == "k" else src[idx]
             for r in range(2):
-                nc.scalar.copy(out=t[:, r, :, :, :], in_=rows[:, r, :].bitcast(F32).rearrange("p (g j u) -> p g u j", g=G, u=2))
+                nc.scalar.copy(out=t[:, r, :, :, :], in_=wk_rows[idx][:, r, :].bitcast(F32).rearrange("p (g j u) -> p g u j", g=G, u=2))
 
         def turn(idx):
-            wg = grp.tile([P, G, 256, 4], BF16, tag="grp", name="wg%d" % idx, align_bytes=64)
+            wg = grp.tile([P, G, ROWS, 4], BF16, tag="grp", name="wg%d" % idx, align_bytes=64)
             groups[idx] = wg
             for r in range(2):
                 for gp in range(2):
-                    tp = psum.tile([P, 2, 2, P], F32, tag="tp", bufs=TPB, name="tpw")
-                    if (r, gp) in WARM_BANKS.get(idx, ()):
-                        nc.tensor.matmul(tp[:].rearrange("p g u c -> p (g u c)"), lhsT=warm_in[:, 0:P], rhs=warm_in[:], start=True, stop=True)
+                    tp = psum.tile([P, 2, 2, P], F32, tag="tp", bufs=TP_BANKS, name="tpw")
+                    if idx >= FIRST_ORDERED - 1 and not contiguous_words(idx) and (r, gp) == (1, 0):
+                        keep_clock(tp[:].rearrange("p g u c -> p (g u c)"))
                     for gg in range(2):
                         g = 2 * gp + gg
                         for u in range(2):
-                            if idx in ORDERED:
+                            if contiguous_words(idx):
                                 nc.tensor.transpose(tp[:, gg, u, :], ordered[idx][:, r, g, u, :], ident[:])
                             else:
-                                rows = rawk[idx] if units[idx][0] == "k" else src[idx]
+                                rows = wk_rows[idx] if UNITS[idx][0] == "k" else wv_rows[idx]
                                 words = rows[:, r, :].bitcast(F32)
                                 nc.tensor.transpose(tp[:, gg, u, :], words[:, 256 * g + u : 256 * (g + 1) : 2], ident[:])
-                    dst = wg[:, 2 * gp : 2 * gp + 2, r * P : (r + 1) * P, :].bitcast(F32)
-                    if (idx in VEC_OUT and gp == 1) or (r, gp) in VEC_BANKS.get(idx, ()):
-                        nc.vector.tensor_copy(out=dst, in_=tp[:].rearrange("p g u c -> p g c u"))
-                    else:
-                        nc.scalar.copy(out=dst, in_=tp[:].rearrange("p g u c -> p g c u"))
-                warm(WARM_UNITS.get(idx, 0))
+                    nc.scalar.copy(out=wg[:, 2 * gp : 2 * gp + 2, r * P : (r + 1) * P, :].bitcast(F32), in_=tp[:].rearrange("p g u c -> p g c u"))
+                if idx < FIRST_ORDERED - 1:
+                    keep_clock_in_free_bank(1)
 
         def quantise(idx):
-            wc = cod.tile([P, G * 256], U32, tag="wc", name="wc%d" % idx, align_bytes=64)
-            ws = cod.tile([P, G * 256], U8, tag="ws", name="ws%d" % idx, align_bytes=64)
+            wc = cod.tile([P, G * ROWS], U32, tag="wc", name="wc%d" % idx, align_bytes=64)
+            ws = cod.tile([P, G * ROWS], U8, tag="ws", name="ws%d" % idx, align_bytes=64)
             nc.vector.quantize_mx(out=wc[:].bitcast(FP8X4), scales=ws[:], in_=groups[idx][:].rearrange("p g c t -> p (g c t)"))
             codes[idx] = (wc, ws)
 
-        def multiply_w(idx):
-            kind, i = units[idx]
+        def multiply_stationary(idx):
+            kind, i = UNITS[idx]
             wc, ws = codes[idx]
             pair = []
             for r in range(2):
                 h = 2 * i + r
-                acc = psum.tile([P, TOK], F32, tag="acc", bufs=ACB, name="acck")
+                acc = psum.tile([P, TOK], F32, tag="acc", bufs=ACC_BANKS, name="acck")
                 for g in range(G):
-                    cols = slice(g * 256 + r * P, g * 256 + (r + 1) * P)
+                    cols = slice(g * ROWS + r * P, g * ROWS + (r + 1) * P)
                     nc.tensor.matmul_mx(
                         out=acc[:],
                         lhsT=wc[:, cols].bitcast(FP8X4),
@@ -264,125 +205,102 @@ def tile_attention_pb_kernel(tc, key_value, wk, bk, wv_bytes, wv_scale, bv, cos,
                         stop=(g == G - 1),
                     )
                 if kind == "k":
-                    rab = rot.tile([P, 2, TOK], F32, tag="rab", name="rab%d" % h)
+                    res = rot.tile([P, 2, TOK], F32, tag="rab", name="rab%d" % h)
                     nc.vector.scalar_tensor_tensor(
-                        out=rab[:],
+                        out=res[:],
                         in0=acc[:].unsqueeze(1).to_broadcast([P, 2, TOK]),
-                        scalar=bias_t[:, h : h + 1],
-                        in1=cs2[:].rearrange("p c b s -> p c (b s)"),
+                        scalar=bias_cols[:, h : h + 1],
+                        in1=cos_sin[:].rearrange("p c b s -> p c (b s)"),
                         op0=ALU.add,
                         op1=ALU.mult,
                     )
                 else:
-                    rab = rot.tile([P, TOK], F32, tag="rab", name="vb%d" % h)
-                    nc.scalar.activation(out=rab[:], in_=acc[:], func=ACT.Identity, bias=bias_t[:, H + h : H + h + 1], scale=1.0)
-                pair.append(rab)
-            rots[idx] = pair
+                    res = rot.tile([P, TOK], F32, tag="rab", name="vb%d" % h)
+                    nc.scalar.activation(out=res[:], in_=acc[:], func=ACT.Identity, bias=bias_cols[:, H + h : H + h + 1], scale=1.0)
+                pair.append(res)
+            turned[idx] = pair
+            to_turn_back.append(idx)
 
-        pending = []
-
-        def back_upto(last):
-            for idx in list(pending):
-                if idx <= last:
-                    pending.remove(idx)
-                    back(idx)
-
-        def back(idx):
-            kind, i = units[idx]
+        def turn_back(idx):
+            kind, i = UNITS[idx]
             for r in range(2):
                 h = 2 * i + r
-                rab = rots[idx][r]
-                ob = psum.tile([P, NB, HD], F32, tag="ob", bufs=OBB, name="ob")
+                res = turned[idx][r]
+                ob = psum.tile([P, NB, HD], F32, tag="ob", bufs=OB_BANKS, name="ob")
                 for b in range(NB):
                     cols = slice(b * S, (b + 1) * S)
                     if kind == "k":
-                        nc.tensor.matmul(ob[:, b, :], lhsT=rab[:, 0, cols], rhs=ident[:], is_transpose=True, start=True, stop=False)
-                        nc.tensor.matmul(ob[:, b, :], lhsT=rab[:, 1, cols], rhs=perm[:], is_transpose=True, start=False, stop=True)
+                        nc.tensor.matmul(ob[:, b, :], lhsT=res[:, 0, cols], rhs=ident[:], is_transpose=True, start=True, stop=False)
+                        nc.tensor.matmul(ob[:, b, :], lhsT=res[:, 1, cols], rhs=perm[:], is_transpose=True, start=False, stop=True)
                     else:
-                        nc.tensor.transpose(ob[:, b, :], rab[:, cols], ident[:])
+                        nc.tensor.transpose(ob[:, b, :], res[:, cols], ident[:])
                 fin = fins.tile([P, NB, HD], F32, tag="fin", name="fink")
                 nc.scalar.copy(out=fin[:], in_=ob[:])
                 dst = out_0 if kind == "k" else out_1
                 nc.sync.dma_start(out=dst[:, h, :, :].rearrange("b s d -> s b d"), in_=fin[:])
 
-        def multiply_v1(idx, b, tag, nbufs):
-            i = units[idx][1]
+        def turn_back_up_to(last):
+            for idx in list(to_turn_back):
+                if idx <= last:
+                    to_turn_back.remove(idx)
+                    turn_back(idx)
+
+        def moving_passes(acc, idx, b):
             wc, ws = codes[idx]
-            acc = psum.tile([P, 256], F32, tag=tag, bufs=nbufs, name="accb")
             for g in range(G):
                 nc.tensor.matmul_mx(
-                    out=acc[:],
+                    out=acc,
                     lhsT=x_codes[:, g, b * S : (b + 1) * S].bitcast(FP8X4),
                     lhsT_scale=x_scales[:, g, b * S : (b + 1) * S],
-                    rhs=wc[:, g * 256 : (g + 1) * 256].bitcast(FP8X4),
-                    rhs_scale=ws[:, g * 256 : (g + 1) * 256],
+                    rhs=wc[:, g * ROWS : (g + 1) * ROWS].bitcast(FP8X4),
+                    rhs_scale=ws[:, g * ROWS : (g + 1) * ROWS],
                     start=(g == 0),
                     stop=(g == G - 1),
                 )
-            fin = fins.tile([P, 256], F32, tag="fin", name="finb")
-            nc.vector.tensor_tensor(out=fin[:], in0=acc[:], in1=bv_b[:, 256 * i : 256 * (i + 1)], op=ALU.add)
-            nc.sync.dma_start(out=out_1[b, 2 * i : 2 * i + 2, :, :].rearrange("h s d -> s h d"), in_=fin[:].rearrange("p (h d) -> p h d", d=HD))
 
-        def multiply_v(idx, halves, tag="acc", nbufs=None):
-            i = units[idx][1]
-            wc, ws = codes[idx]
-            for bp in halves:
-                acc = psum.tile([P, 2, 256], F32, tag=tag, bufs=nbufs or ACB, name="accv")
+        def store_values(i, b, fin):
+            nc.sync.dma_start(out=out_1[b, 2 * i : 2 * i + 2, :, :].rearrange("h s d -> s h d"), in_=fin.rearrange("p (h d) -> p h d", d=HD))
+
+        def multiply_moving(idx):
+            i = UNITS[idx][1]
+            for bp in range(2):
+                acc = psum.tile([P, 2, ROWS], F32, tag="acc", bufs=ACC_BANKS, name="accv")
                 for bb in range(2):
-                    b = 2 * bp + bb
-                    for g in range(G):
-                        nc.tensor.matmul_mx(
-                            out=acc[:, bb, :],
-                            lhsT=x_codes[:, g, b * S : (b + 1) * S].bitcast(FP8X4),
-                            lhsT_scale=x_scales[:, g, b * S : (b + 1) * S],
-                            rhs=wc[:, g * 256 : (g + 1) * 256].bitcast(FP8X4),
-                            rhs_scale=ws[:, g * 256 : (g + 1) * 256],
-                            start=(g == 0),
-                            stop=(g == G - 1),
-                        )
-                fin = fins.tile([P, 2, 256], F32, tag="fin", name="finv")
+                    moving_passes(acc[:, bb, :], idx, 2 * bp + bb)
+                fin = fins.tile([P, 2, ROWS], F32, tag="fin", name="finv")
                 nc.vector.tensor_tensor(
                     out=fin[:],
                     in0=acc[:],
-                    in1=bv_b[:, 256 * i : 256 * (i + 1)].unsqueeze(1).to_broadcast([P, 2, 256]),
+                    in1=bv_b[:, ROWS * i : ROWS * (i + 1)].unsqueeze(1).to_broadcast([P, 2, ROWS]),
                     op=ALU.add,
                 )
                 for bb in range(2):
-                    b = 2 * bp + bb
-                    nc.sync.dma_start(
-                        out=out_1[b, 2 * i : 2 * i + 2, :, :].rearrange("h s d -> s h d"),
-                        in_=fin[:, bb, :].rearrange("p (h d) -> p h d", d=HD),
-                    )
+                    store_values(i, 2 * bp + bb, fin[:, bb, :])
 
-        def spread_bv(q):
-            tpb = psum.tile([P, 4, P], F32, tag="tp", bufs=TPB, name="tpb")
-            for mm in range(4):
-                h = 4 * q + mm
-                nc.tensor.transpose(tpb[:, mm, :], bias_t[:, H + h : H + h + 1].to_broadcast([P, P]), ident[:])
-            nc.scalar.copy(out=bv_b[:, 512 * q : 512 * (q + 1)], in_=tpb[:].rearrange("p m r -> p (m r)"))
+        def multiply_moving_one_batch(idx, b):
+            i = UNITS[idx][1]
+            acc = psum.tile([P, ROWS], F32, tag="tp", bufs=TP_BANKS, name="accb")
+            moving_passes(acc[:], idx, b)
+            fin = fins.tile([P, ROWS], F32, tag="fin", name="finb")
+            nc.vector.tensor_tensor(out=fin[:], in0=acc[:], in1=bv_b[:, ROWS * i : ROWS * (i + 1)], op=ALU.add)
+            store_values(i, b, fin[:])
 
-        next_products(PIECES[0], 4 if CHUNK_FIRST else 1)
-        if LATE_CONST:
-            constants()
+        next_products(2)
 
         xg = []
         for gp in range(2):
             xg_t = grp.tile([P, 2, TOK, 4], BF16, tag="grp", name="xg%d" % gp, align_bytes=64)
             xg.append(xg_t)
         for b in range(NB):
-            words = xr[b // 2][:, b % 2, :].bitcast(F32)
+            words = x_rows[b // 2][:, b % 2, :].bitcast(F32)
             for gp in range(2):
-                tp = psum.tile([P, 2, 2, P], F32, tag="tp", bufs=TPB, name="tpx")
+                tp = psum.tile([P, 2, 2, P], F32, tag="tp", bufs=TP_BANKS, name="tpx")
                 for gg in range(2):
                     g = 2 * gp + gg
                     for u in range(2):
                         nc.tensor.transpose(tp[:, gg, u, :], words[:, 256 * g + u : 256 * (g + 1) : 2], ident[:])
-                dst = xg[gp][:, :, b * P : (b + 1) * P, :].bitcast(F32)
-                if (b, gp) in XVEC:
-                    nc.vector.tensor_copy(out=dst, in_=tp[:].rearrange("p g u c -> p g c u"))
-                else:
-                    nc.scalar.copy(out=dst, in_=tp[:].rearrange("p g u c -> p g c u"))
-            warm(WARM_X if b in WARM_XB else 0)
+                nc.scalar.copy(out=xg[gp][:, :, b * P : (b + 1) * P, :].bitcast(F32), in_=tp[:].rearrange("p g u c -> p g c u"))
+            keep_clock_in_free_bank(1)
         for gp in range(2):
             nc.vector.quantize_mx(
                 out=x_codes[:, 2 * gp : 2 * gp + 2, :].rearrange("p g c -> p (g c)").bitcast(FP8X4),
@@ -393,50 +311,38 @@ def tile_attention_pb_kernel(tc, key_value, wk, bk, wv_bytes, wv_scale, bv, cos,
         turn(0)
         quantise(0)
 
-        cst = const.tile([P, 3, P], F32, name="cst")
-        tpc = psum.tile([P, 4, P], F32, tag="tp", bufs=TPB, name="tpc")
+        tables = const.tile([P, 3, P], F32, name="tables")
+        tpc = psum.tile([P, 4, P], F32, tag="tp", bufs=TP_BANKS, name="tpc")
         nc.tensor.transpose(tpc[:, 0, :], csf[:, 0, :], ident[:])
         nc.tensor.transpose(tpc[:, 1, :], csf[:, 1, :], ident[:])
         nc.tensor.transpose(tpc[:, 2, :], b_f[:], ident[:])
-        nc.scalar.copy(out=cst[:], in_=tpc[:, 0:3, :])
-        bias_t = cst[:, 2, :]
-        cs2 = const.tile([P, 2, NB, S], F32, name="cs2")
-        if BV == "pe" and -1 in BV_AT:
-            spread_bv(BV_AT[-1])
+        nc.scalar.copy(out=tables[:], in_=tpc[:, 0:3, :])
+        bias_cols = tables[:, 2, :]
+        cos_sin = const.tile([P, 2, NB, S], F32, name="cos_sin")
 
-        for j in range(n_units):
-            if len(loaded) < n_units:
-                load_next()
-            if BV_SLOT == j:
+        for j in range(N_UNITS):
+            if len(loaded) < N_UNITS:
+                load(len(loaded))
+            if j == 1:
                 nc.sync.dma_start(out=bv_b[:], in_=bv.partition_broadcast(P))
-            next_products(PIECES[j + 1] if j + 1 < len(PIECES) else 0)
-            if BACK_FIRST and j < n_units - 1:
-                back_upto(j - BACK)
-            if j + 1 < n_units:
+            next_products(1)
+            if j + 1 < N_UNITS:
                 turn(j + 1)
             if j == 0:
-                nc.scalar.copy(out=cs2[:], in_=cst[:, 0:2, :].unsqueeze(2).to_broadcast([P, 2, NB, S]))
-            if BV == "pe" and j in BV_AT:
-                spread_bv(BV_AT[j])
-            if j + ORDER_AHEAD in ORDERED:
-                permute(j + ORDER_AHEAD)
-            if j + 1 < n_units:
+                nc.scalar.copy(out=cos_sin[:], in_=tables[:, 0:2, :].unsqueeze(2).to_broadcast([P, 2, NB, S]))
+            if j + 2 < N_UNITS and contiguous_words(j + 2):
+                order_words(j + 2)
+            if j + 1 < N_UNITS:
                 quantise(j + 1)
-            if j == n_units - 1:
-                tg, nb = ("tp", TPB) if LAST_TP else ("acc", ACB)
-                for step in LAST_ORDER.split():
-                    if step == "back":
-                        back_upto(j)
-                    elif LAST_SPLIT:
-                        multiply_v1(j, 2 * int(step[1]), tg, nb)
-                        multiply_v1(j, 2 * int(step[1]) + 1, tg, nb)
-                    else:
-                        multiply_v(j, (int(step[1]),), tg, nb)
-            else:
-                if not BACK_FIRST:
-                    back_upto(j - BACK)
-                if units[j][0] == "v":
-                    multiply_v(j, (0, 1))
+            if j < N_UNITS - 1:
+                turn_back_up_to(j - 2)
+                if UNITS[j][0] == "v":
+                    multiply_moving(j)
                 else:
-                    multiply_w(j)
-                    pending.append(j)
+                    multiply_stationary(j)
+            else:
+                multiply_moving_one_batch(j, 0)
+                multiply_moving_one_batch(j, 1)
+                turn_back_up_to(j)
+                multiply_moving_one_batch(j, 2)
+                multiply_moving_one_batch(j, 3)

@@ -16,47 +16,74 @@ NB, S, DIM, H, HD = 4, 128, 2048, 16, 128
 P = 128
 G = DIM // 512
 TOK = NB * S
-ROWS = 2 * HD
 FLOPS = 2 * TOK * DIM * 2 * H * HD
 
-UNITS = (
-    ("s", 0), ("k", 0), ("k", 1), ("v", 1), ("k", 2), ("v", 2), ("k", 3), ("v", 3),
-    ("k", 4), ("v", 4), ("k", 5), ("v", 5), ("k", 6), ("v", 6), ("k", 7), ("v", 7),
-)
-N_UNITS = len(UNITS)
-FIRST_ORDERED = 4
-FIRST_LOADS = (3, 1, 2, 4)
-TP_BANKS, ACC_BANKS, OB_BANKS = 4, 2, 2
+UNITS = (("s", 0), ("k", 0), ("k", 1), ("v", 1), ("k", 2), ("v", 2), ("k", 3), ("v", 3), ("k", 4), ("v", 4), ("k", 5), ("v", 5), ("k", 6), ("v", 6), ("k", 7), ("v", 7))
+ORDERED = (4, 6, 8, 10, 12, 14)
+ORDER_AHEAD = 2
+PIECES = (2, 1, 1, 1, 1, 1, 1, 1, 1, 1, 1, 1, 1, 1, 1)
+LOOKAHEAD = 5
+FIRST_LOADS = (0, "x", 3, 1, 2, 4)
+BV = "dma"
+BV_AT = {}
+SCALE_OUT = "vector"
+CHUNK_FIRST = False
+BACK = 2
+BACK_FIRST = False
+BUFS = {"raw": 5, "vby": 4, "vbf": 4, "prm": 3, "grp": 3, "cod": 3, "rot": 4, "fins": 6, "tp": 4, "acc": 2, "ob": 2}
+VEC_OUT = ()
+LATE_CONST = False
+BV_SLOT = 1
+XVEC = ()
+VEC_BANKS = {}
+LAST_TP = True
+LAST_SPLIT = True
+LAST_ORDER = "h0 back h1"
+WARM_START = 6
+WARM_SCALE = 3
+WARM_X = 1
+WARM_XB = (0, 1, 2, 3)
+WARM_UNITS = {0: 1, 1: 1, 2: 1}
+WARM_BANKS = {3: ((1, 0),), 5: ((1, 0),), 7: ((1, 0),), 9: ((1, 0),), 11: ((1, 0),), 13: ((1, 0),), 15: ((1, 0),)}
+PAIRED = False
+V_IN_TP = False
+PAIR_PIECES = (1, 1)
+PAIR_BACK = "mid"
+HALVES = None
+WARM_N = 384
+WHOLE = 99
 
 
 def tile_attention_pb_kernel(tc, key_value, wk, bk, wv_bytes, wv_scale, bv, cos, sin, out_0, out_1):
     nc = tc.nc
     with ExitStack() as ctx:
         const = ctx.enter_context(tc.tile_pool(name="const", bufs=1))
-        raw = ctx.enter_context(tc.tile_pool(name="raw", bufs=5))
-        vby = ctx.enter_context(tc.tile_pool(name="vby", bufs=4))
-        vbf = ctx.enter_context(tc.tile_pool(name="vbf", bufs=4))
-        prm = ctx.enter_context(tc.tile_pool(name="prm", bufs=3))
-        grp = ctx.enter_context(tc.tile_pool(name="grp", bufs=3))
-        cod = ctx.enter_context(tc.tile_pool(name="cod", bufs=3))
-        rot = ctx.enter_context(tc.tile_pool(name="rot", bufs=4))
-        fins = ctx.enter_context(tc.tile_pool(name="fins", bufs=6))
+        raw = ctx.enter_context(tc.tile_pool(name="raw", bufs=BUFS["raw"]))
+        vby = ctx.enter_context(tc.tile_pool(name="vby", bufs=BUFS["vby"]))
+        vbf = ctx.enter_context(tc.tile_pool(name="vbf", bufs=BUFS["vbf"]))
+        prm = ctx.enter_context(tc.tile_pool(name="prm", bufs=BUFS["prm"]))
+        grp = ctx.enter_context(tc.tile_pool(name="grp", bufs=BUFS["grp"]))
+        cod = ctx.enter_context(tc.tile_pool(name="cod", bufs=BUFS["cod"]))
+        rot = ctx.enter_context(tc.tile_pool(name="rot", bufs=BUFS["rot"]))
+        fins = ctx.enter_context(tc.tile_pool(name="fins", bufs=BUFS["fins"]))
         psum = ctx.enter_context(tc.psum_pool(name="psum", bufs=2))
         ctx.enter_context(tc.manual_schedule())
 
-        zeros = const.tile([P, TOK], BF16, name="zeros")
-        nc.vector.memset(zeros[:], 0.0)
+        units = UNITS
+        n_units = len(units)
+        TPB, ACB, OBB = BUFS["tp"], BUFS["acc"], BUFS["ob"]
 
-        def keep_clock(bank):
-            nc.tensor.matmul(bank, lhsT=zeros[:, 0:P], rhs=zeros[:], start=True, stop=True)
+        warm_in = const.tile([P, TOK], BF16, name="warm_in")
+        if WARM_START + WARM_SCALE + WARM_X + len(WARM_UNITS) + len(WARM_BANKS) > 0:
+            nc.vector.memset(warm_in[:], 0.0)
 
-        def keep_clock_in_free_bank(count):
-            bank = psum.tile([P, TOK], F32, tag="acc", bufs=ACC_BANKS, name="idle")
-            for c in range(count):
-                keep_clock(bank[:])
+        def warm(count):
+            if count > 0:
+                wps = psum.tile([P, TOK], F32, tag="acc", bufs=BUFS["acc"], name="wps")
+                for c in range(count):
+                    nc.tensor.matmul(wps[:, 0:WARM_N], lhsT=warm_in[:, 0:P], rhs=warm_in[:, 0:WARM_N], start=True, stop=True)
 
-        keep_clock_in_free_bank(6)
-
+        warm(WARM_START)
         s_raw = const.tile([P, P], F32, name="s_raw")
         nc.gpsimd.memset(s_raw[:], 0.0)
         b_raw = const.tile([P, P], BF16, name="b_raw")
@@ -65,136 +92,202 @@ def tile_attention_pb_kernel(tc, key_value, wk, bk, wv_bytes, wv_scale, bv, cos,
         make_identity(nc, ident[:])
         cs_raw = const.tile([P, 2, P], BF16, name="cs_raw")
         nc.sync.dma_start(out=s_raw[0:16, :], in_=wv_scale.rearrange("o (m p) -> (o m) p", p=P))
-        nc.sync.dma_start(out=cs_raw[:, 0, :], in_=cos.rearrange("a b s d -> (a b s) d"))
-        nc.sync.dma_start(out=cs_raw[:, 1, :], in_=sin.rearrange("a b s d -> (a b s) d"))
-        nc.sync.dma_start(out=b_raw[0:H, :], in_=bk.rearrange("(h d) -> h d", d=HD))
-        nc.sync.dma_start(out=b_raw[H : 2 * H, :], in_=bv.rearrange("(h d) -> h d", d=HD))
 
-        scale_b = const.tile([P, DIM], F32, name="scale_b")
+        def small_loads():
+            nc.sync.dma_start(out=cs_raw[:, 0, :], in_=cos.rearrange("a b s d -> (a b s) d"))
+            nc.sync.dma_start(out=cs_raw[:, 1, :], in_=sin.rearrange("a b s d -> (a b s) d"))
+            nc.sync.dma_start(out=b_raw[0:H, :], in_=bk.rearrange("(h d) -> h d", d=HD))
+            nc.sync.dma_start(out=b_raw[H : 2 * H, :], in_=bv.rearrange("(h d) -> h d", d=HD))
+
+        if "small" not in FIRST_LOADS:
+            small_loads()
+
+        scale_2 = const.tile([P, 2, DIM], F32, name="scale_2")
+        scale_b = scale_2[:, 0, :]
         bv_b = const.tile([P, H * HD], BF16, name="bv_b")
 
-        wk_rows = {}
-        wv_codes_in = {}
-        wv_rows = {}
-        loaded = []
+        src = {}
+        byt = {}
+        rawk = {}
+        xr = []
 
         def load(idx):
-            kind, i = UNITS[idx]
-            rows = slice(ROWS * i, ROWS * (i + 1))
+            kind, i = units[idx]
+            rows = slice(256 * i, 256 * (i + 1))
             if kind == "k":
                 t = raw.tile([P, 2, DIM], BF16, tag="raw", name="wkr%d" % i)
                 nc.sync.dma_start(out=t[:], in_=wk[rows, :].rearrange("(r p) k -> p r k", p=P))
-                wk_rows[idx] = t
+                rawk[idx] = t
             else:
                 t = vby.tile([P, 2, DIM], U8, tag="vby", name="wvy%d" % i)
                 nc.sync.dma_start(out=t[:], in_=wv_bytes[rows, :].rearrange("(r p) k -> p r k", p=P))
-                wv_codes_in[idx] = t
-            loaded.append(idx)
+                byt[idx] = t
 
-        load(0)
-        x_rows = []
+        loaded = []
         for j in range(2):
-            x_t = raw.tile([P, 2, DIM], BF16, tag="raw", name="xr%d" % j)
-            x_rows.append(x_t)
-        for b in range(NB):
-            nc.sync.dma_start(out=x_rows[b // 2][:, b % 2, :], in_=key_value[b])
-        for idx in FIRST_LOADS:
-            load(idx)
+            xr_t = raw.tile([P, 2, DIM], BF16, tag="raw", name="xr%d" % j)
+            xr.append(xr_t)
+        for what in FIRST_LOADS:
+            if what == "x":
+                for b in range(NB):
+                    nc.sync.dma_start(out=xr[b // 2][:, b % 2, :], in_=key_value[b])
+            elif what in ("x0", "x1", "x2", "x3"):
+                b = int(what[1])
+                nc.sync.dma_start(out=xr[b // 2][:, b % 2, :], in_=key_value[b])
+            elif what == "small":
+                small_loads()
+            elif what == "bv":
+                nc.sync.dma_start(out=bv_b[:], in_=bv.partition_broadcast(P))
+            else:
+                load(what)
+                loaded.append(what)
+
+        def load_next():
+            for idx in range(n_units):
+                if idx not in loaded:
+                    load(idx)
+                    loaded.append(idx)
+                    return
 
         perm = const.tile([P, P], F32, name="perm")
         csf = const.tile([P, 2, P], F32, name="csf")
         b_f = const.tile([P, P], F32, name="b_f")
-        nc.vector.tensor_copy(out=perm[:, 0:64], in_=ident[:, 64:128])
-        nc.vector.tensor_copy(out=perm[:, 64:128], in_=ident[:, 0:64])
-        nc.vector.tensor_copy(out=csf[:, 0, :], in_=cs_raw[:, 0, :])
-        nc.vector.tensor_copy(out=csf[:, 1, 0:64], in_=cs_raw[:, 1, 64:128])
-        nc.vector.tensor_scalar(out=csf[:, 1, 64:128], in0=cs_raw[:, 1, 0:64], scalar1=-1.0, scalar2=None, op0=ALU.mult)
-        nc.vector.tensor_copy(out=b_f[:], in_=b_raw[:])
+
+        def constants():
+            nc.vector.tensor_copy(out=perm[:, 0:64], in_=ident[:, 64:128])
+            nc.vector.tensor_copy(out=perm[:, 64:128], in_=ident[:, 0:64])
+            nc.vector.tensor_copy(out=csf[:, 0, :], in_=cs_raw[:, 0, :])
+            nc.vector.tensor_copy(out=csf[:, 1, 0:64], in_=cs_raw[:, 1, 64:128])
+            nc.vector.tensor_scalar(out=csf[:, 1, 64:128], in0=cs_raw[:, 1, 0:64], scalar1=-1.0, scalar2=None, op0=ALU.mult)
+            nc.vector.tensor_copy(out=b_f[:], in_=b_raw[:])
+
+        if not LATE_CONST:
+            constants()
 
         scol = const.tile([P, 16], F32, name="scol")
-        tp0 = psum.tile([P, NB, S], F32, tag="tp", bufs=TP_BANKS, name="tp0")
+        tp0 = psum.tile([P, NB, S], F32, tag="tp", bufs=TPB, name="tp0")
         nc.tensor.transpose(tp0[:, 0, :], s_raw[:], ident[:])
         nc.scalar.copy(out=scol[:], in_=tp0[:, 0, 0:16])
         for q in range(4):
-            tpq = psum.tile([P, 4, P], F32, tag="tp", bufs=TP_BANKS, name="tpq")
+            tpq = psum.tile([P, 4, P], F32, tag="tp", bufs=TPB, name="tpq")
             for mm in range(4):
                 m = 4 * q + mm
                 nc.tensor.transpose(tpq[:, mm, :], scol[:, m : m + 1].to_broadcast([P, P]), ident[:])
-            nc.vector.tensor_copy(out=scale_b[:, 512 * q : 512 * (q + 1)], in_=tpq[:].rearrange("p m r -> p (m r)"))
-        keep_clock_in_free_bank(3)
+            if SCALE_OUT == "vector" or (SCALE_OUT == "both" and q % 2 == 1):
+                nc.vector.tensor_copy(out=scale_b[:, 512 * q : 512 * (q + 1)], in_=tpq[:].rearrange("p m r -> p (m r)"))
+            else:
+                nc.scalar.copy(out=scale_b[:, 512 * q : 512 * (q + 1)], in_=tpq[:].rearrange("p m r -> p (m r)"))
+            if WHOLE < 99:
+                nc.scalar.copy(out=scale_2[:, 1, 512 * q : 512 * (q + 1)], in_=tpq[:].rearrange("p m r -> p (m r)"))
 
+        warm(WARM_SCALE)
         x_codes = const.tile([P, G, TOK], U32, name="x_codes", align_bytes=64)
         x_scales = const.tile([P, G, TOK], U8, name="x_scales", align_bytes=64)
 
-        ordered = {}
-        groups = {}
         codes = {}
-        turned = {}
-        to_turn_back = []
+        rots = {}
+        groups = {}
+        ordered = {}
 
-        def product(idx, r):
+        def product(idx, r, chunks=1):
             if r == 0:
                 t = vbf.tile([P, 2, DIM], BF16, tag="vbf", name="wvb%d" % idx)
-                wv_rows[idx] = t
-            nc.vector.tensor_tensor(out=wv_rows[idx][:, r, :], in0=wv_codes_in[idx][:, r, :].bitcast(FP8), in1=scale_b[:], op=ALU.mult)
+                src[idx] = t
+            w = DIM // chunks
+            for c in range(chunks):
+                cols = slice(c * w, (c + 1) * w)
+                nc.vector.tensor_tensor(out=src[idx][:, r, cols], in0=byt[idx][:, r, cols].bitcast(FP8), in1=scale_b[:, cols], op=ALU.mult)
 
-        row_tiles = []
-        for idx in range(N_UNITS):
-            if UNITS[idx][0] != "k":
-                row_tiles.append((idx, 0))
-                row_tiles.append((idx, 1))
+        pieces = []
+        for idx in range(n_units):
+            if units[idx][0] != "k":
+                pieces.append((idx, 0))
+                pieces.append((idx, 1))
 
-        def next_products(count):
+        def product2(idx):
+            t = vbf.tile([P, 2, DIM], BF16, tag="vbf", name="wvb%d" % idx)
+            src[idx] = t
+            nc.vector.tensor_tensor(
+                out=t[:].rearrange("p r k -> p (r k)"),
+                in0=byt[idx][:].rearrange("p r k -> p (r k)").bitcast(FP8),
+                in1=scale_2[:].rearrange("p r k -> p (r k)"),
+                op=ALU.mult,
+            )
+
+        half_left = []
+
+        def first_half():
+            if len(pieces) > 0:
+                idx, r = pieces.pop(0)
+                if r == 0:
+                    t = vbf.tile([P, 2, DIM], BF16, tag="vbf", name="wvb%d" % idx)
+                    src[idx] = t
+                cols = slice(0, DIM // 2)
+                nc.vector.tensor_tensor(out=src[idx][:, r, cols], in0=byt[idx][:, r, cols].bitcast(FP8), in1=scale_b[:, cols], op=ALU.mult)
+                half_left.append((idx, r))
+
+        def second_half():
+            if len(half_left) > 0:
+                idx, r = half_left.pop(0)
+                cols = slice(DIM // 2, DIM)
+                nc.vector.tensor_tensor(out=src[idx][:, r, cols], in0=byt[idx][:, r, cols].bitcast(FP8), in1=scale_b[:, cols], op=ALU.mult)
+
+        def next_products(count, chunks=1):
             for c in range(count):
-                if len(row_tiles) > 0:
-                    idx, r = row_tiles.pop(0)
-                    product(idx, r)
+                if len(pieces) > 0:
+                    idx, r = pieces.pop(0)
+                    if 16 - len(pieces) - 1 >= WHOLE:
+                        if r == 0:
+                            product2(idx)
+                    else:
+                        product(idx, r, chunks if c == 0 else 1)
 
-        def contiguous_words(idx):
-            return UNITS[idx][0] == "k" and idx >= FIRST_ORDERED
-
-        def order_words(idx):
+        def permute(idx):
             t = prm.tile([P, 2, G, 2, P], F32, tag="prm", name="wkp%d" % idx)
             ordered[idx] = t
+            rows = rawk[idx] if units[idx][0] == "k" else src[idx]
             for r in range(2):
-                nc.scalar.copy(out=t[:, r, :, :, :], in_=wk_rows[idx][:, r, :].bitcast(F32).rearrange("p (g j u) -> p g u j", g=G, u=2))
+                nc.scalar.copy(out=t[:, r, :, :, :], in_=rows[:, r, :].bitcast(F32).rearrange("p (g j u) -> p g u j", g=G, u=2))
 
         def turn(idx):
-            wg = grp.tile([P, G, ROWS, 4], BF16, tag="grp", name="wg%d" % idx, align_bytes=64)
+            wg = grp.tile([P, G, 256, 4], BF16, tag="grp", name="wg%d" % idx, align_bytes=64)
             groups[idx] = wg
             for r in range(2):
                 for gp in range(2):
-                    tp = psum.tile([P, 2, 2, P], F32, tag="tp", bufs=TP_BANKS, name="tpw")
-                    if idx >= FIRST_ORDERED - 1 and not contiguous_words(idx) and (r, gp) == (1, 0):
-                        keep_clock(tp[:].rearrange("p g u c -> p (g u c)"))
+                    tp = psum.tile([P, 2, 2, P], F32, tag="tp", bufs=TPB, name="tpw")
+                    if (r, gp) in WARM_BANKS.get(idx, ()):
+                        nc.tensor.matmul(tp[:].rearrange("p g u c -> p (g u c)")[:, 0:WARM_N], lhsT=warm_in[:, 0:P], rhs=warm_in[:, 0:WARM_N], start=True, stop=True)
                     for gg in range(2):
                         g = 2 * gp + gg
                         for u in range(2):
-                            if contiguous_words(idx):
+                            if idx in ORDERED:
                                 nc.tensor.transpose(tp[:, gg, u, :], ordered[idx][:, r, g, u, :], ident[:])
                             else:
-                                rows = wk_rows[idx] if UNITS[idx][0] == "k" else wv_rows[idx]
+                                rows = rawk[idx] if units[idx][0] == "k" else src[idx]
                                 words = rows[:, r, :].bitcast(F32)
                                 nc.tensor.transpose(tp[:, gg, u, :], words[:, 256 * g + u : 256 * (g + 1) : 2], ident[:])
-                    nc.scalar.copy(out=wg[:, 2 * gp : 2 * gp + 2, r * P : (r + 1) * P, :].bitcast(F32), in_=tp[:].rearrange("p g u c -> p g c u"))
-                if idx < FIRST_ORDERED - 1:
-                    keep_clock_in_free_bank(1)
+                    dst = wg[:, 2 * gp : 2 * gp + 2, r * P : (r + 1) * P, :].bitcast(F32)
+                    if (idx in VEC_OUT and gp == 1) or (r, gp) in VEC_BANKS.get(idx, ()):
+                        nc.vector.tensor_copy(out=dst, in_=tp[:].rearrange("p g u c -> p g c u"))
+                    else:
+                        nc.scalar.copy(out=dst, in_=tp[:].rearrange("p g u c -> p g c u"))
+                warm(WARM_UNITS.get(idx, 0))
 
         def quantise(idx):
-            wc = cod.tile([P, G * ROWS], U32, tag="wc", name="wc%d" % idx, align_bytes=64)
-            ws = cod.tile([P, G * ROWS], U8, tag="ws", name="ws%d" % idx, align_bytes=64)
+            wc = cod.tile([P, G * 256], U32, tag="wc", name="wc%d" % idx, align_bytes=64)
+            ws = cod.tile([P, G * 256], U8, tag="ws", name="ws%d" % idx, align_bytes=64)
             nc.vector.quantize_mx(out=wc[:].bitcast(FP8X4), scales=ws[:], in_=groups[idx][:].rearrange("p g c t -> p (g c t)"))
             codes[idx] = (wc, ws)
 
-        def multiply_stationary(idx):
-            kind, i = UNITS[idx]
+        def multiply_w(idx):
+            kind, i = units[idx]
             wc, ws = codes[idx]
             pair = []
             for r in range(2):
                 h = 2 * i + r
-                acc = psum.tile([P, TOK], F32, tag="acc", bufs=ACC_BANKS, name="acck")
+                acc = psum.tile([P, TOK], F32, tag="acc", bufs=ACB, name="acck")
                 for g in range(G):
-                    cols = slice(g * ROWS + r * P, g * ROWS + (r + 1) * P)
+                    cols = slice(g * 256 + r * P, g * 256 + (r + 1) * P)
                     nc.tensor.matmul_mx(
                         out=acc[:],
                         lhsT=wc[:, cols].bitcast(FP8X4),
@@ -205,102 +298,125 @@ def tile_attention_pb_kernel(tc, key_value, wk, bk, wv_bytes, wv_scale, bv, cos,
                         stop=(g == G - 1),
                     )
                 if kind == "k":
-                    res = rot.tile([P, 2, TOK], F32, tag="rab", name="rab%d" % h)
+                    rab = rot.tile([P, 2, TOK], F32, tag="rab", name="rab%d" % h)
                     nc.vector.scalar_tensor_tensor(
-                        out=res[:],
+                        out=rab[:],
                         in0=acc[:].unsqueeze(1).to_broadcast([P, 2, TOK]),
-                        scalar=bias_cols[:, h : h + 1],
-                        in1=cos_sin[:].rearrange("p c b s -> p c (b s)"),
+                        scalar=bias_t[:, h : h + 1],
+                        in1=cs2[:].rearrange("p c b s -> p c (b s)"),
                         op0=ALU.add,
                         op1=ALU.mult,
                     )
                 else:
-                    res = rot.tile([P, TOK], F32, tag="rab", name="vb%d" % h)
-                    nc.scalar.activation(out=res[:], in_=acc[:], func=ACT.Identity, bias=bias_cols[:, H + h : H + h + 1], scale=1.0)
-                pair.append(res)
-            turned[idx] = pair
-            to_turn_back.append(idx)
+                    rab = rot.tile([P, TOK], F32, tag="rab", name="vb%d" % h)
+                    nc.scalar.activation(out=rab[:], in_=acc[:], func=ACT.Identity, bias=bias_t[:, H + h : H + h + 1], scale=1.0)
+                pair.append(rab)
+            rots[idx] = pair
 
-        def turn_back(idx):
-            kind, i = UNITS[idx]
+        pending = []
+
+        def back_upto(last):
+            for idx in list(pending):
+                if idx <= last:
+                    pending.remove(idx)
+                    back(idx)
+
+        def back(idx):
+            kind, i = units[idx]
             for r in range(2):
                 h = 2 * i + r
-                res = turned[idx][r]
-                ob = psum.tile([P, NB, HD], F32, tag="ob", bufs=OB_BANKS, name="ob")
+                rab = rots[idx][r]
+                ob = psum.tile([P, NB, HD], F32, tag="ob", bufs=OBB, name="ob")
                 for b in range(NB):
                     cols = slice(b * S, (b + 1) * S)
                     if kind == "k":
-                        nc.tensor.matmul(ob[:, b, :], lhsT=res[:, 0, cols], rhs=ident[:], is_transpose=True, start=True, stop=False)
-                        nc.tensor.matmul(ob[:, b, :], lhsT=res[:, 1, cols], rhs=perm[:], is_transpose=True, start=False, stop=True)
+                        nc.tensor.matmul(ob[:, b, :], lhsT=rab[:, 0, cols], rhs=ident[:], is_transpose=True, start=True, stop=False)
+                        nc.tensor.matmul(ob[:, b, :], lhsT=rab[:, 1, cols], rhs=perm[:], is_transpose=True, start=False, stop=True)
                     else:
-                        nc.tensor.transpose(ob[:, b, :], res[:, cols], ident[:])
+                        nc.tensor.transpose(ob[:, b, :], rab[:, cols], ident[:])
                 fin = fins.tile([P, NB, HD], F32, tag="fin", name="fink")
                 nc.scalar.copy(out=fin[:], in_=ob[:])
                 dst = out_0 if kind == "k" else out_1
                 nc.sync.dma_start(out=dst[:, h, :, :].rearrange("b s d -> s b d"), in_=fin[:])
 
-        def turn_back_up_to(last):
-            for idx in list(to_turn_back):
-                if idx <= last:
-                    to_turn_back.remove(idx)
-                    turn_back(idx)
-
-        def moving_passes(acc, idx, b):
+        def multiply_v1(idx, b, tag, nbufs):
+            i = units[idx][1]
             wc, ws = codes[idx]
+            acc = psum.tile([P, 256], F32, tag=tag, bufs=nbufs, name="accb")
             for g in range(G):
                 nc.tensor.matmul_mx(
-                    out=acc,
+                    out=acc[:],
                     lhsT=x_codes[:, g, b * S : (b + 1) * S].bitcast(FP8X4),
                     lhsT_scale=x_scales[:, g, b * S : (b + 1) * S],
-                    rhs=wc[:, g * ROWS : (g + 1) * ROWS].bitcast(FP8X4),
-                    rhs_scale=ws[:, g * ROWS : (g + 1) * ROWS],
+                    rhs=wc[:, g * 256 : (g + 1) * 256].bitcast(FP8X4),
+                    rhs_scale=ws[:, g * 256 : (g + 1) * 256],
                     start=(g == 0),
                     stop=(g == G - 1),
                 )
+            fin = fins.tile([P, 256], F32, tag="fin", name="finb")
+            nc.vector.tensor_tensor(out=fin[:], in0=acc[:], in1=bv_b[:, 256 * i : 256 * (i + 1)], op=ALU.add)
+            nc.sync.dma_start(out=out_1[b, 2 * i : 2 * i + 2, :, :].rearrange("h s d -> s h d"), in_=fin[:].rearrange("p (h d) -> p h d", d=HD))
 
-        def store_values(i, b, fin):
-            nc.sync.dma_start(out=out_1[b, 2 * i : 2 * i + 2, :, :].rearrange("h s d -> s h d"), in_=fin.rearrange("p (h d) -> p h d", d=HD))
-
-        def multiply_moving(idx):
-            i = UNITS[idx][1]
-            for bp in range(2):
-                acc = psum.tile([P, 2, ROWS], F32, tag="acc", bufs=ACC_BANKS, name="accv")
+        def multiply_v(idx, halves, tag="acc", nbufs=None):
+            i = units[idx][1]
+            wc, ws = codes[idx]
+            for bp in halves:
+                acc = psum.tile([P, 2, 256], F32, tag=tag, bufs=nbufs or ACB, name="accv")
                 for bb in range(2):
-                    moving_passes(acc[:, bb, :], idx, 2 * bp + bb)
-                fin = fins.tile([P, 2, ROWS], F32, tag="fin", name="finv")
+                    b = 2 * bp + bb
+                    for g in range(G):
+                        nc.tensor.matmul_mx(
+                            out=acc[:, bb, :],
+                            lhsT=x_codes[:, g, b * S : (b + 1) * S].bitcast(FP8X4),
+                            lhsT_scale=x_scales[:, g, b * S : (b + 1) * S],
+                            rhs=wc[:, g * 256 : (g + 1) * 256].bitcast(FP8X4),
+                            rhs_scale=ws[:, g * 256 : (g + 1) * 256],
+                            start=(g == 0),
+                            stop=(g == G - 1),
+                        )
+                fin = fins.tile([P, 2, 256], F32, tag="fin", name="finv")
                 nc.vector.tensor_tensor(
                     out=fin[:],
                     in0=acc[:],
-                    in1=bv_b[:, ROWS * i : ROWS * (i + 1)].unsqueeze(1).to_broadcast([P, 2, ROWS]),
+                    in1=bv_b[:, 256 * i : 256 * (i + 1)].unsqueeze(1).to_broadcast([P, 2, 256]),
                     op=ALU.add,
                 )
                 for bb in range(2):
-                    store_values(i, 2 * bp + bb, fin[:, bb, :])
+                    b = 2 * bp + bb
+                    nc.sync.dma_start(
+                        out=out_1[b, 2 * i : 2 * i + 2, :, :].rearrange("h s d -> s h d"),
+                        in_=fin[:, bb, :].rearrange("p (h d) -> p h d", d=HD),
+                    )
 
-        def multiply_moving_one_batch(idx, b):
-            i = UNITS[idx][1]
-            acc = psum.tile([P, ROWS], F32, tag="tp", bufs=TP_BANKS, name="accb")
-            moving_passes(acc[:], idx, b)
-            fin = fins.tile([P, ROWS], F32, tag="fin", name="finb")
-            nc.vector.tensor_tensor(out=fin[:], in0=acc[:], in1=bv_b[:, ROWS * i : ROWS * (i + 1)], op=ALU.add)
-            store_values(i, b, fin[:])
+        def spread_bv(q):
+            tpb = psum.tile([P, 4, P], F32, tag="tp", bufs=TPB, name="tpb")
+            for mm in range(4):
+                h = 4 * q + mm
+                nc.tensor.transpose(tpb[:, mm, :], bias_t[:, H + h : H + h + 1].to_broadcast([P, P]), ident[:])
+            nc.scalar.copy(out=bv_b[:, 512 * q : 512 * (q + 1)], in_=tpb[:].rearrange("p m r -> p (m r)"))
 
-        next_products(2)
+        next_products(PIECES[0], 4 if CHUNK_FIRST else 1)
+        if LATE_CONST:
+            constants()
 
         xg = []
         for gp in range(2):
             xg_t = grp.tile([P, 2, TOK, 4], BF16, tag="grp", name="xg%d" % gp, align_bytes=64)
             xg.append(xg_t)
         for b in range(NB):
-            words = x_rows[b // 2][:, b % 2, :].bitcast(F32)
+            words = xr[b // 2][:, b % 2, :].bitcast(F32)
             for gp in range(2):
-                tp = psum.tile([P, 2, 2, P], F32, tag="tp", bufs=TP_BANKS, name="tpx")
+                tp = psum.tile([P, 2, 2, P], F32, tag="tp", bufs=TPB, name="tpx")
                 for gg in range(2):
                     g = 2 * gp + gg
                     for u in range(2):
                         nc.tensor.transpose(tp[:, gg, u, :], words[:, 256 * g + u : 256 * (g + 1) : 2], ident[:])
-                nc.scalar.copy(out=xg[gp][:, :, b * P : (b + 1) * P, :].bitcast(F32), in_=tp[:].rearrange("p g u c -> p g c u"))
-            keep_clock_in_free_bank(1)
+                dst = xg[gp][:, :, b * P : (b + 1) * P, :].bitcast(F32)
+                if (b, gp) in XVEC:
+                    nc.vector.tensor_copy(out=dst, in_=tp[:].rearrange("p g u c -> p g c u"))
+                else:
+                    nc.scalar.copy(out=dst, in_=tp[:].rearrange("p g u c -> p g c u"))
+            warm(WARM_X if b in WARM_XB else 0)
         for gp in range(2):
             nc.vector.quantize_mx(
                 out=x_codes[:, 2 * gp : 2 * gp + 2, :].rearrange("p g c -> p (g c)").bitcast(FP8X4),
@@ -311,38 +427,107 @@ def tile_attention_pb_kernel(tc, key_value, wk, bk, wv_bytes, wv_scale, bv, cos,
         turn(0)
         quantise(0)
 
-        tables = const.tile([P, 3, P], F32, name="tables")
-        tpc = psum.tile([P, 4, P], F32, tag="tp", bufs=TP_BANKS, name="tpc")
+        cst = const.tile([P, 3, P], F32, name="cst")
+        tpc = psum.tile([P, 4, P], F32, tag="tp", bufs=TPB, name="tpc")
         nc.tensor.transpose(tpc[:, 0, :], csf[:, 0, :], ident[:])
         nc.tensor.transpose(tpc[:, 1, :], csf[:, 1, :], ident[:])
         nc.tensor.transpose(tpc[:, 2, :], b_f[:], ident[:])
-        nc.scalar.copy(out=tables[:], in_=tpc[:, 0:3, :])
-        bias_cols = tables[:, 2, :]
-        cos_sin = const.tile([P, 2, NB, S], F32, name="cos_sin")
+        nc.scalar.copy(out=cst[:], in_=tpc[:, 0:3, :])
+        bias_t = cst[:, 2, :]
+        cs2 = const.tile([P, 2, NB, S], F32, name="cs2")
+        if BV == "pe" and -1 in BV_AT:
+            spread_bv(BV_AT[-1])
 
-        for j in range(N_UNITS):
-            if len(loaded) < N_UNITS:
-                load(len(loaded))
-            if j == 1:
+        def multiply(idx):
+            if units[idx][0] == "v":
+                if V_IN_TP:
+                    multiply_v(idx, (0, 1), "tp", TPB)
+                else:
+                    multiply_v(idx, (0, 1))
+            else:
+                multiply_w(idx)
+                pending.append(idx)
+
+        for p in range(n_units // 2 if PAIRED else 0):
+            a = 2 * p
+            b = a + 1
+            for c in range(2):
+                if len(loaded) < n_units:
+                    load_next()
+            if BV_SLOT == p:
                 nc.sync.dma_start(out=bv_b[:], in_=bv.partition_broadcast(P))
-            next_products(1)
-            if j + 1 < N_UNITS:
+            next_products(PAIR_PIECES[0])
+            if PAIR_BACK == "first":
+                back_upto(a - 1)
+            turn(b)
+            if p == 0:
+                nc.scalar.copy(out=cs2[:], in_=cst[:, 0:2, :].unsqueeze(2).to_broadcast([P, 2, NB, S]))
+            quantise(b)
+            if PAIR_BACK == "mid":
+                back_upto(a - 1)
+            next_products(PAIR_PIECES[1])
+            if a + 2 < n_units:
+                turn(a + 2)
+            if PAIR_BACK == "last":
+                back_upto(a - 1)
+            if a + 4 in ORDERED:
+                permute(a + 4)
+            if a + 2 < n_units:
+                quantise(a + 2)
+            multiply(a)
+            if b < n_units - 1:
+                multiply(b)
+            else:
+                tg, nb = ("tp", TPB) if LAST_TP else ("acc", ACB)
+                for step in LAST_ORDER.split():
+                    if step == "back":
+                        back_upto(b)
+                    elif LAST_SPLIT:
+                        multiply_v1(b, 2 * int(step[1]), tg, nb)
+                        multiply_v1(b, 2 * int(step[1]) + 1, tg, nb)
+                    else:
+                        multiply_v(b, (int(step[1]),), tg, nb)
+
+        for j in range(0 if PAIRED else n_units):
+            if len(loaded) < n_units:
+                load_next()
+            if BV_SLOT == j:
+                nc.sync.dma_start(out=bv_b[:], in_=bv.partition_broadcast(P))
+            if HALVES is None:
+                next_products(PIECES[j + 1] if j + 1 < len(PIECES) else 0)
+            else:
+                first_half()
+            if BACK_FIRST and j < n_units - 1:
+                back_upto(j - BACK)
+            if j + 1 < n_units:
                 turn(j + 1)
             if j == 0:
-                nc.scalar.copy(out=cos_sin[:], in_=tables[:, 0:2, :].unsqueeze(2).to_broadcast([P, 2, NB, S]))
-            if j + 2 < N_UNITS and contiguous_words(j + 2):
-                order_words(j + 2)
-            if j + 1 < N_UNITS:
+                nc.scalar.copy(out=cs2[:], in_=cst[:, 0:2, :].unsqueeze(2).to_broadcast([P, 2, NB, S]))
+            if BV == "pe" and j in BV_AT:
+                spread_bv(BV_AT[j])
+            if j + ORDER_AHEAD in ORDERED:
+                permute(j + ORDER_AHEAD)
+            if j + 1 < n_units:
                 quantise(j + 1)
-            if j < N_UNITS - 1:
-                turn_back_up_to(j - 2)
-                if UNITS[j][0] == "v":
-                    multiply_moving(j)
-                else:
-                    multiply_stationary(j)
+            if HALVES == "after_q":
+                second_half()
+            if j == n_units - 1:
+                tg, nb = ("tp", TPB) if LAST_TP else ("acc", ACB)
+                for step in LAST_ORDER.split():
+                    if step == "back":
+                        back_upto(j)
+                    elif LAST_SPLIT:
+                        multiply_v1(j, 2 * int(step[1]), tg, nb)
+                        multiply_v1(j, 2 * int(step[1]) + 1, tg, nb)
+                    else:
+                        multiply_v(j, (int(step[1]),), tg, nb)
             else:
-                multiply_moving_one_batch(j, 0)
-                multiply_moving_one_batch(j, 1)
-                turn_back_up_to(j)
-                multiply_moving_one_batch(j, 2)
-                multiply_moving_one_batch(j, 3)
+                if not BACK_FIRST:
+                    back_upto(j - BACK)
+                if units[j][0] == "v":
+                    multiply_v(j, (0, 1))
+                else:
+                    multiply_w(j)
+                    pending.append(j)
+            if HALVES == "after_mul":
+                second_half()

@@ -16,74 +16,52 @@ NB, S, DIM, H, HD = 4, 128, 2048, 16, 128
 P = 128
 G = DIM // 512
 TOK = NB * S
+ROWS = 2 * HD
 FLOPS = 2 * TOK * DIM * 2 * H * HD
 
-UNITS = (("s", 0), ("k", 0), ("k", 1), ("v", 1), ("k", 2), ("v", 2), ("k", 3), ("v", 3), ("k", 4), ("v", 4), ("k", 5), ("v", 5), ("k", 6), ("v", 6), ("k", 7), ("v", 7))
-ORDERED = (4, 6, 8, 10, 12, 14)
-ORDER_AHEAD = 2
-PIECES = (2, 1, 1, 1, 1, 1, 1, 1, 1, 1, 1, 1, 1, 1, 1)
-LOOKAHEAD = 5
-FIRST_LOADS = (0, "x", 3, 1, 2, 4)
-BV = "dma"
-BV_AT = {}
-SCALE_OUT = "vector"
-CHUNK_FIRST = False
-BACK = 2
-BACK_FIRST = False
-BUFS = {"raw": 5, "vby": 4, "vbf": 4, "prm": 3, "grp": 3, "cod": 3, "rot": 4, "fins": 6, "tp": 4, "acc": 2, "ob": 2}
-VEC_OUT = ()
-LATE_CONST = False
-BV_SLOT = 1
-XVEC = ()
-VEC_BANKS = {}
-LAST_TP = True
-LAST_SPLIT = True
-LAST_ORDER = "h0 back h1"
-WARM_START = 6
-WARM_SCALE = 3
-WARM_X = 1
-WARM_XB = (0, 1, 2, 3)
-WARM_UNITS = {0: 1, 1: 1, 2: 1}
-WARM_BANKS = {3: ((1, 0),), 5: ((1, 0),), 7: ((1, 0),), 9: ((1, 0),), 11: ((1, 0),), 13: ((1, 0),), 15: ((1, 0),)}
-PAIRED = False
-V_IN_TP = False
-PAIR_PIECES = (1, 1)
-PAIR_BACK = "mid"
-HALVES = None
-WARM_N = 384
-WHOLE = 99
+UNITS = (
+    ("s", 0), ("k", 0), ("k", 1), ("v", 1), ("k", 2), ("v", 2), ("k", 3), ("v", 3),
+    ("k", 4), ("v", 4), ("k", 5), ("v", 5), ("k", 6), ("v", 6), ("k", 7), ("v", 7),
+)
+N_UNITS = len(UNITS)
+FIRST_ORDERED = 4
+FIRST_LOADS = (3, 1, 2, 4)
+TP_BANKS, ACC_BANKS, OB_BANKS = 4, 2, 2
+CLOCK_COLUMNS = 256
+IDLE_AT_START, IDLE_BEFORE_KEY_VALUE = 6, 3
+FIRST_BETWEEN_PASSES = 3
+BANK = 512
+WORDS = 256
 
 
 def tile_attention_pb_kernel(tc, key_value, wk, bk, wv_bytes, wv_scale, bv, cos, sin, out_0, out_1):
     nc = tc.nc
     with ExitStack() as ctx:
         const = ctx.enter_context(tc.tile_pool(name="const", bufs=1))
-        raw = ctx.enter_context(tc.tile_pool(name="raw", bufs=BUFS["raw"]))
-        vby = ctx.enter_context(tc.tile_pool(name="vby", bufs=BUFS["vby"]))
-        vbf = ctx.enter_context(tc.tile_pool(name="vbf", bufs=BUFS["vbf"]))
-        prm = ctx.enter_context(tc.tile_pool(name="prm", bufs=BUFS["prm"]))
-        grp = ctx.enter_context(tc.tile_pool(name="grp", bufs=BUFS["grp"]))
-        cod = ctx.enter_context(tc.tile_pool(name="cod", bufs=BUFS["cod"]))
-        rot = ctx.enter_context(tc.tile_pool(name="rot", bufs=BUFS["rot"]))
-        fins = ctx.enter_context(tc.tile_pool(name="fins", bufs=BUFS["fins"]))
+        raw = ctx.enter_context(tc.tile_pool(name="raw", bufs=5))
+        vby = ctx.enter_context(tc.tile_pool(name="vby", bufs=4))
+        vbf = ctx.enter_context(tc.tile_pool(name="vbf", bufs=4))
+        prm = ctx.enter_context(tc.tile_pool(name="prm", bufs=3))
+        grp = ctx.enter_context(tc.tile_pool(name="grp", bufs=3))
+        cod = ctx.enter_context(tc.tile_pool(name="cod", bufs=3))
+        rot = ctx.enter_context(tc.tile_pool(name="rot", bufs=4))
+        fins = ctx.enter_context(tc.tile_pool(name="fins", bufs=6))
         psum = ctx.enter_context(tc.psum_pool(name="psum", bufs=2))
         ctx.enter_context(tc.manual_schedule())
 
-        units = UNITS
-        n_units = len(units)
-        TPB, ACB, OBB = BUFS["tp"], BUFS["acc"], BUFS["ob"]
+        zeros = const.tile([P, TOK], BF16, name="zeros")
+        nc.vector.memset(zeros[:], 0.0)
 
-        warm_in = const.tile([P, TOK], BF16, name="warm_in")
-        if WARM_START + WARM_SCALE + WARM_X + len(WARM_UNITS) + len(WARM_BANKS) > 0:
-            nc.vector.memset(warm_in[:], 0.0)
+        def keep_clock(bank):
+            nc.tensor.matmul(bank[:, 0:CLOCK_COLUMNS], lhsT=zeros[:, 0:P], rhs=zeros[:, 0:CLOCK_COLUMNS], start=True, stop=True)
 
-        def warm(count):
-            if count > 0:
-                wps = psum.tile([P, TOK], F32, tag="acc", bufs=BUFS["acc"], name="wps")
-                for c in range(count):
-                    nc.tensor.matmul(wps[:, 0:WARM_N], lhsT=warm_in[:, 0:P], rhs=warm_in[:, 0:WARM_N], start=True, stop=True)
+        def keep_clock_in_free_bank(count):
+            bank = psum.tile([P, TOK], F32, tag="acc", bufs=ACC_BANKS, name="idle")
+            for c in range(count):
+                keep_clock(bank[:])
 
-        warm(WARM_START)
+        keep_clock_in_free_bank(IDLE_AT_START)
+
         s_raw = const.tile([P, P], F32, name="s_raw")
         nc.gpsimd.memset(s_raw[:], 0.0)
         b_raw = const.tile([P, P], BF16, name="b_raw")
@@ -91,203 +69,137 @@ def tile_attention_pb_kernel(tc, key_value, wk, bk, wv_bytes, wv_scale, bv, cos,
         ident = const.tile([P, P], F32, name="ident")
         make_identity(nc, ident[:])
         cs_raw = const.tile([P, 2, P], BF16, name="cs_raw")
-        nc.sync.dma_start(out=s_raw[0:16, :], in_=wv_scale.rearrange("o (m p) -> (o m) p", p=P))
+        nc.sync.dma_start(out=s_raw[0 : DIM // P, :], in_=wv_scale.rearrange("o (m p) -> (o m) p", p=P))
+        nc.sync.dma_start(out=cs_raw[:, 0, :], in_=cos.rearrange("a b s d -> (a b s) d"))
+        nc.sync.dma_start(out=cs_raw[:, 1, :], in_=sin.rearrange("a b s d -> (a b s) d"))
+        nc.sync.dma_start(out=b_raw[0:H, :], in_=bk.rearrange("(h d) -> h d", d=HD))
+        nc.sync.dma_start(out=b_raw[H : 2 * H, :], in_=bv.rearrange("(h d) -> h d", d=HD))
 
-        def small_loads():
-            nc.sync.dma_start(out=cs_raw[:, 0, :], in_=cos.rearrange("a b s d -> (a b s) d"))
-            nc.sync.dma_start(out=cs_raw[:, 1, :], in_=sin.rearrange("a b s d -> (a b s) d"))
-            nc.sync.dma_start(out=b_raw[0:H, :], in_=bk.rearrange("(h d) -> h d", d=HD))
-            nc.sync.dma_start(out=b_raw[H : 2 * H, :], in_=bv.rearrange("(h d) -> h d", d=HD))
-
-        if "small" not in FIRST_LOADS:
-            small_loads()
-
-        scale_2 = const.tile([P, 2, DIM], F32, name="scale_2")
-        scale_b = scale_2[:, 0, :]
+        scale_b = const.tile([P, DIM], F32, name="scale_b")
         bv_b = const.tile([P, H * HD], BF16, name="bv_b")
 
-        src = {}
-        byt = {}
-        rawk = {}
-        xr = []
+        wk_rows = {}
+        wv_bytes_in = {}
+        wv_rows = {}
+        loaded = []
 
         def load(idx):
-            kind, i = units[idx]
-            rows = slice(256 * i, 256 * (i + 1))
+            kind, i = UNITS[idx]
+            span = slice(ROWS * i, ROWS * (i + 1))
             if kind == "k":
-                t = raw.tile([P, 2, DIM], BF16, tag="raw", name="wkr%d" % i)
-                nc.sync.dma_start(out=t[:], in_=wk[rows, :].rearrange("(r p) k -> p r k", p=P))
-                rawk[idx] = t
+                wkr = raw.tile([P, 2, DIM], BF16, tag="raw", name="wkr%d" % i)
+                nc.sync.dma_start(out=wkr[:], in_=wk[span, :].rearrange("(r p) k -> p r k", p=P))
+                wk_rows[idx] = wkr
             else:
-                t = vby.tile([P, 2, DIM], U8, tag="vby", name="wvy%d" % i)
-                nc.sync.dma_start(out=t[:], in_=wv_bytes[rows, :].rearrange("(r p) k -> p r k", p=P))
-                byt[idx] = t
+                wvy = vby.tile([P, 2, DIM], U8, tag="vby", name="wvy%d" % i)
+                nc.sync.dma_start(out=wvy[:], in_=wv_bytes[span, :].rearrange("(r p) k -> p r k", p=P))
+                wv_bytes_in[idx] = wvy
+            loaded.append(idx)
 
-        loaded = []
+        load(0)
+        x_rows = []
         for j in range(2):
-            xr_t = raw.tile([P, 2, DIM], BF16, tag="raw", name="xr%d" % j)
-            xr.append(xr_t)
-        for what in FIRST_LOADS:
-            if what == "x":
-                for b in range(NB):
-                    nc.sync.dma_start(out=xr[b // 2][:, b % 2, :], in_=key_value[b])
-            elif what in ("x0", "x1", "x2", "x3"):
-                b = int(what[1])
-                nc.sync.dma_start(out=xr[b // 2][:, b % 2, :], in_=key_value[b])
-            elif what == "small":
-                small_loads()
-            elif what == "bv":
-                nc.sync.dma_start(out=bv_b[:], in_=bv.partition_broadcast(P))
-            else:
-                load(what)
-                loaded.append(what)
-
-        def load_next():
-            for idx in range(n_units):
-                if idx not in loaded:
-                    load(idx)
-                    loaded.append(idx)
-                    return
+            x_t = raw.tile([P, 2, DIM], BF16, tag="raw", name="xr%d" % j)
+            x_rows.append(x_t)
+        for b in range(NB):
+            nc.sync.dma_start(out=x_rows[b // 2][:, b % 2, :], in_=key_value[b])
+        for idx in FIRST_LOADS:
+            load(idx)
 
         perm = const.tile([P, P], F32, name="perm")
         csf = const.tile([P, 2, P], F32, name="csf")
         b_f = const.tile([P, P], F32, name="b_f")
+        nc.vector.tensor_copy(out=perm[:, 0:64], in_=ident[:, 64:128])
+        nc.vector.tensor_copy(out=perm[:, 64:128], in_=ident[:, 0:64])
+        nc.vector.tensor_copy(out=csf[:, 0, :], in_=cs_raw[:, 0, :])
+        nc.vector.tensor_copy(out=csf[:, 1, 0:64], in_=cs_raw[:, 1, 64:128])
+        nc.vector.tensor_scalar(out=csf[:, 1, 64:128], in0=cs_raw[:, 1, 0:64], scalar1=-1.0, scalar2=None, op0=ALU.mult)
+        nc.vector.tensor_copy(out=b_f[:], in_=b_raw[:])
 
-        def constants():
-            nc.vector.tensor_copy(out=perm[:, 0:64], in_=ident[:, 64:128])
-            nc.vector.tensor_copy(out=perm[:, 64:128], in_=ident[:, 0:64])
-            nc.vector.tensor_copy(out=csf[:, 0, :], in_=cs_raw[:, 0, :])
-            nc.vector.tensor_copy(out=csf[:, 1, 0:64], in_=cs_raw[:, 1, 64:128])
-            nc.vector.tensor_scalar(out=csf[:, 1, 64:128], in0=cs_raw[:, 1, 0:64], scalar1=-1.0, scalar2=None, op0=ALU.mult)
-            nc.vector.tensor_copy(out=b_f[:], in_=b_raw[:])
-
-        if not LATE_CONST:
-            constants()
-
-        scol = const.tile([P, 16], F32, name="scol")
-        tp0 = psum.tile([P, NB, S], F32, tag="tp", bufs=TPB, name="tp0")
+        scol = const.tile([P, DIM // P], F32, name="scol")
+        tp0 = psum.tile([P, NB, S], F32, tag="tp", bufs=TP_BANKS, name="tp0")
         nc.tensor.transpose(tp0[:, 0, :], s_raw[:], ident[:])
-        nc.scalar.copy(out=scol[:], in_=tp0[:, 0, 0:16])
+        nc.scalar.copy(out=scol[:], in_=tp0[:, 0, 0 : DIM // P])
         for q in range(4):
-            tpq = psum.tile([P, 4, P], F32, tag="tp", bufs=TPB, name="tpq")
+            tpq = psum.tile([P, 4, P], F32, tag="tp", bufs=TP_BANKS, name="tpq")
             for mm in range(4):
                 m = 4 * q + mm
                 nc.tensor.transpose(tpq[:, mm, :], scol[:, m : m + 1].to_broadcast([P, P]), ident[:])
-            if SCALE_OUT == "vector" or (SCALE_OUT == "both" and q % 2 == 1):
-                nc.vector.tensor_copy(out=scale_b[:, 512 * q : 512 * (q + 1)], in_=tpq[:].rearrange("p m r -> p (m r)"))
-            else:
-                nc.scalar.copy(out=scale_b[:, 512 * q : 512 * (q + 1)], in_=tpq[:].rearrange("p m r -> p (m r)"))
-            if WHOLE < 99:
-                nc.scalar.copy(out=scale_2[:, 1, 512 * q : 512 * (q + 1)], in_=tpq[:].rearrange("p m r -> p (m r)"))
+            nc.vector.tensor_copy(out=scale_b[:, BANK * q : BANK * (q + 1)], in_=tpq[:].rearrange("p m r -> p (m r)"))
+        keep_clock_in_free_bank(IDLE_BEFORE_KEY_VALUE)
 
-        warm(WARM_SCALE)
         x_codes = const.tile([P, G, TOK], U32, name="x_codes", align_bytes=64)
         x_scales = const.tile([P, G, TOK], U8, name="x_scales", align_bytes=64)
 
-        codes = {}
-        rots = {}
-        groups = {}
         ordered = {}
+        groups = {}
+        codes = {}
+        by_feature = {}
+        to_turn_back = []
 
-        def product(idx, r, chunks=1):
+        def product(idx, r):
             if r == 0:
-                t = vbf.tile([P, 2, DIM], BF16, tag="vbf", name="wvb%d" % idx)
-                src[idx] = t
-            w = DIM // chunks
-            for c in range(chunks):
-                cols = slice(c * w, (c + 1) * w)
-                nc.vector.tensor_tensor(out=src[idx][:, r, cols], in0=byt[idx][:, r, cols].bitcast(FP8), in1=scale_b[:, cols], op=ALU.mult)
+                wvb = vbf.tile([P, 2, DIM], BF16, tag="vbf", name="wvb%d" % idx)
+                wv_rows[idx] = wvb
+            nc.vector.tensor_tensor(out=wv_rows[idx][:, r, :], in0=wv_bytes_in[idx][:, r, :].bitcast(FP8), in1=scale_b[:], op=ALU.mult)
 
-        pieces = []
-        for idx in range(n_units):
-            if units[idx][0] != "k":
-                pieces.append((idx, 0))
-                pieces.append((idx, 1))
+        row_tiles = []
+        for idx in range(N_UNITS):
+            if UNITS[idx][0] != "k":
+                row_tiles.append((idx, 0))
+                row_tiles.append((idx, 1))
 
-        def product2(idx):
-            t = vbf.tile([P, 2, DIM], BF16, tag="vbf", name="wvb%d" % idx)
-            src[idx] = t
-            nc.vector.tensor_tensor(
-                out=t[:].rearrange("p r k -> p (r k)"),
-                in0=byt[idx][:].rearrange("p r k -> p (r k)").bitcast(FP8),
-                in1=scale_2[:].rearrange("p r k -> p (r k)"),
-                op=ALU.mult,
-            )
-
-        half_left = []
-
-        def first_half():
-            if len(pieces) > 0:
-                idx, r = pieces.pop(0)
-                if r == 0:
-                    t = vbf.tile([P, 2, DIM], BF16, tag="vbf", name="wvb%d" % idx)
-                    src[idx] = t
-                cols = slice(0, DIM // 2)
-                nc.vector.tensor_tensor(out=src[idx][:, r, cols], in0=byt[idx][:, r, cols].bitcast(FP8), in1=scale_b[:, cols], op=ALU.mult)
-                half_left.append((idx, r))
-
-        def second_half():
-            if len(half_left) > 0:
-                idx, r = half_left.pop(0)
-                cols = slice(DIM // 2, DIM)
-                nc.vector.tensor_tensor(out=src[idx][:, r, cols], in0=byt[idx][:, r, cols].bitcast(FP8), in1=scale_b[:, cols], op=ALU.mult)
-
-        def next_products(count, chunks=1):
+        def next_products(count):
             for c in range(count):
-                if len(pieces) > 0:
-                    idx, r = pieces.pop(0)
-                    if 16 - len(pieces) - 1 >= WHOLE:
-                        if r == 0:
-                            product2(idx)
-                    else:
-                        product(idx, r, chunks if c == 0 else 1)
+                if len(row_tiles) > 0:
+                    idx, r = row_tiles.pop(0)
+                    product(idx, r)
 
-        def permute(idx):
-            t = prm.tile([P, 2, G, 2, P], F32, tag="prm", name="wkp%d" % idx)
-            ordered[idx] = t
-            rows = rawk[idx] if units[idx][0] == "k" else src[idx]
+        def contiguous_words(idx):
+            return UNITS[idx][0] == "k" and idx >= FIRST_ORDERED
+
+        def order_words(idx):
+            wkp = prm.tile([P, 2, G, 2, P], F32, tag="prm", name="wkp%d" % idx)
+            ordered[idx] = wkp
             for r in range(2):
-                nc.scalar.copy(out=t[:, r, :, :, :], in_=rows[:, r, :].bitcast(F32).rearrange("p (g j u) -> p g u j", g=G, u=2))
+                nc.scalar.copy(out=wkp[:, r, :, :, :], in_=wk_rows[idx][:, r, :].bitcast(F32).rearrange("p (g j u) -> p g u j", g=G, u=2))
 
         def turn(idx):
-            wg = grp.tile([P, G, 256, 4], BF16, tag="grp", name="wg%d" % idx, align_bytes=64)
+            wg = grp.tile([P, G, ROWS, 4], BF16, tag="grp", name="wg%d" % idx, align_bytes=64)
             groups[idx] = wg
             for r in range(2):
                 for gp in range(2):
-                    tp = psum.tile([P, 2, 2, P], F32, tag="tp", bufs=TPB, name="tpw")
-                    if (r, gp) in WARM_BANKS.get(idx, ()):
-                        nc.tensor.matmul(tp[:].rearrange("p g u c -> p (g u c)")[:, 0:WARM_N], lhsT=warm_in[:, 0:P], rhs=warm_in[:, 0:WARM_N], start=True, stop=True)
+                    tp = psum.tile([P, 2, 2, P], F32, tag="tp", bufs=TP_BANKS, name="tpw")
+                    if idx >= FIRST_BETWEEN_PASSES and not contiguous_words(idx) and (r, gp) == (1, 0):
+                        keep_clock(tp[:].rearrange("p g u c -> p (g u c)"))
                     for gg in range(2):
                         g = 2 * gp + gg
                         for u in range(2):
-                            if idx in ORDERED:
+                            if contiguous_words(idx):
                                 nc.tensor.transpose(tp[:, gg, u, :], ordered[idx][:, r, g, u, :], ident[:])
                             else:
-                                rows = rawk[idx] if units[idx][0] == "k" else src[idx]
+                                rows = wk_rows[idx] if UNITS[idx][0] == "k" else wv_rows[idx]
                                 words = rows[:, r, :].bitcast(F32)
-                                nc.tensor.transpose(tp[:, gg, u, :], words[:, 256 * g + u : 256 * (g + 1) : 2], ident[:])
-                    dst = wg[:, 2 * gp : 2 * gp + 2, r * P : (r + 1) * P, :].bitcast(F32)
-                    if (idx in VEC_OUT and gp == 1) or (r, gp) in VEC_BANKS.get(idx, ()):
-                        nc.vector.tensor_copy(out=dst, in_=tp[:].rearrange("p g u c -> p g c u"))
-                    else:
-                        nc.scalar.copy(out=dst, in_=tp[:].rearrange("p g u c -> p g c u"))
-                warm(WARM_UNITS.get(idx, 0))
+                                nc.tensor.transpose(tp[:, gg, u, :], words[:, WORDS * g + u : WORDS * (g + 1) : 2], ident[:])
+                    nc.scalar.copy(out=wg[:, 2 * gp : 2 * gp + 2, r * P : (r + 1) * P, :].bitcast(F32), in_=tp[:].rearrange("p g u c -> p g c u"))
+                if idx < FIRST_BETWEEN_PASSES:
+                    keep_clock_in_free_bank(1)
 
         def quantise(idx):
-            wc = cod.tile([P, G * 256], U32, tag="wc", name="wc%d" % idx, align_bytes=64)
-            ws = cod.tile([P, G * 256], U8, tag="ws", name="ws%d" % idx, align_bytes=64)
+            wc = cod.tile([P, G * ROWS], U32, tag="wc", name="wc%d" % idx, align_bytes=64)
+            ws = cod.tile([P, G * ROWS], U8, tag="ws", name="ws%d" % idx, align_bytes=64)
             nc.vector.quantize_mx(out=wc[:].bitcast(FP8X4), scales=ws[:], in_=groups[idx][:].rearrange("p g c t -> p (g c t)"))
             codes[idx] = (wc, ws)
 
-        def multiply_w(idx):
-            kind, i = units[idx]
+        def multiply_stationary(idx):
+            kind, i = UNITS[idx]
             wc, ws = codes[idx]
             pair = []
             for r in range(2):
                 h = 2 * i + r
-                acc = psum.tile([P, TOK], F32, tag="acc", bufs=ACB, name="acck")
+                acc = psum.tile([P, TOK], F32, tag="acc", bufs=ACC_BANKS, name="acck")
                 for g in range(G):
-                    cols = slice(g * 256 + r * P, g * 256 + (r + 1) * P)
+                    cols = slice(g * ROWS + r * P, g * ROWS + (r + 1) * P)
                     nc.tensor.matmul_mx(
                         out=acc[:],
                         lhsT=wc[:, cols].bitcast(FP8X4),
@@ -298,125 +210,102 @@ def tile_attention_pb_kernel(tc, key_value, wk, bk, wv_bytes, wv_scale, bv, cos,
                         stop=(g == G - 1),
                     )
                 if kind == "k":
-                    rab = rot.tile([P, 2, TOK], F32, tag="rab", name="rab%d" % h)
+                    res = rot.tile([P, 2, TOK], F32, tag="rab", name="rab%d" % h)
                     nc.vector.scalar_tensor_tensor(
-                        out=rab[:],
+                        out=res[:],
                         in0=acc[:].unsqueeze(1).to_broadcast([P, 2, TOK]),
-                        scalar=bias_t[:, h : h + 1],
-                        in1=cs2[:].rearrange("p c b s -> p c (b s)"),
+                        scalar=bias_cols[:, h : h + 1],
+                        in1=cos_sin[:].rearrange("p c b s -> p c (b s)"),
                         op0=ALU.add,
                         op1=ALU.mult,
                     )
                 else:
-                    rab = rot.tile([P, TOK], F32, tag="rab", name="vb%d" % h)
-                    nc.scalar.activation(out=rab[:], in_=acc[:], func=ACT.Identity, bias=bias_t[:, H + h : H + h + 1], scale=1.0)
-                pair.append(rab)
-            rots[idx] = pair
+                    res = rot.tile([P, TOK], F32, tag="rab", name="vb%d" % h)
+                    nc.scalar.activation(out=res[:], in_=acc[:], func=ACT.Identity, bias=bias_cols[:, H + h : H + h + 1], scale=1.0)
+                pair.append(res)
+            by_feature[idx] = pair
+            to_turn_back.append(idx)
 
-        pending = []
-
-        def back_upto(last):
-            for idx in list(pending):
-                if idx <= last:
-                    pending.remove(idx)
-                    back(idx)
-
-        def back(idx):
-            kind, i = units[idx]
+        def turn_back(idx):
+            kind, i = UNITS[idx]
             for r in range(2):
                 h = 2 * i + r
-                rab = rots[idx][r]
-                ob = psum.tile([P, NB, HD], F32, tag="ob", bufs=OBB, name="ob")
+                res = by_feature[idx][r]
+                ob = psum.tile([P, NB, HD], F32, tag="ob", bufs=OB_BANKS, name="ob")
                 for b in range(NB):
                     cols = slice(b * S, (b + 1) * S)
                     if kind == "k":
-                        nc.tensor.matmul(ob[:, b, :], lhsT=rab[:, 0, cols], rhs=ident[:], is_transpose=True, start=True, stop=False)
-                        nc.tensor.matmul(ob[:, b, :], lhsT=rab[:, 1, cols], rhs=perm[:], is_transpose=True, start=False, stop=True)
+                        nc.tensor.matmul(ob[:, b, :], lhsT=res[:, 0, cols], rhs=ident[:], is_transpose=True, start=True, stop=False)
+                        nc.tensor.matmul(ob[:, b, :], lhsT=res[:, 1, cols], rhs=perm[:], is_transpose=True, start=False, stop=True)
                     else:
-                        nc.tensor.transpose(ob[:, b, :], rab[:, cols], ident[:])
+                        nc.tensor.transpose(ob[:, b, :], res[:, cols], ident[:])
                 fin = fins.tile([P, NB, HD], F32, tag="fin", name="fink")
                 nc.scalar.copy(out=fin[:], in_=ob[:])
                 dst = out_0 if kind == "k" else out_1
                 nc.sync.dma_start(out=dst[:, h, :, :].rearrange("b s d -> s b d"), in_=fin[:])
 
-        def multiply_v1(idx, b, tag, nbufs):
-            i = units[idx][1]
+        def turn_back_up_to(last):
+            for idx in list(to_turn_back):
+                if idx <= last:
+                    to_turn_back.remove(idx)
+                    turn_back(idx)
+
+        def moving_passes(acc, idx, b):
             wc, ws = codes[idx]
-            acc = psum.tile([P, 256], F32, tag=tag, bufs=nbufs, name="accb")
             for g in range(G):
                 nc.tensor.matmul_mx(
-                    out=acc[:],
+                    out=acc,
                     lhsT=x_codes[:, g, b * S : (b + 1) * S].bitcast(FP8X4),
                     lhsT_scale=x_scales[:, g, b * S : (b + 1) * S],
-                    rhs=wc[:, g * 256 : (g + 1) * 256].bitcast(FP8X4),
-                    rhs_scale=ws[:, g * 256 : (g + 1) * 256],
+                    rhs=wc[:, g * ROWS : (g + 1) * ROWS].bitcast(FP8X4),
+                    rhs_scale=ws[:, g * ROWS : (g + 1) * ROWS],
                     start=(g == 0),
                     stop=(g == G - 1),
                 )
-            fin = fins.tile([P, 256], F32, tag="fin", name="finb")
-            nc.vector.tensor_tensor(out=fin[:], in0=acc[:], in1=bv_b[:, 256 * i : 256 * (i + 1)], op=ALU.add)
-            nc.sync.dma_start(out=out_1[b, 2 * i : 2 * i + 2, :, :].rearrange("h s d -> s h d"), in_=fin[:].rearrange("p (h d) -> p h d", d=HD))
 
-        def multiply_v(idx, halves, tag="acc", nbufs=None):
-            i = units[idx][1]
-            wc, ws = codes[idx]
-            for bp in halves:
-                acc = psum.tile([P, 2, 256], F32, tag=tag, bufs=nbufs or ACB, name="accv")
+        def store_values(i, b, fin):
+            nc.sync.dma_start(out=out_1[b, 2 * i : 2 * i + 2, :, :].rearrange("h s d -> s h d"), in_=fin.rearrange("p (h d) -> p h d", d=HD))
+
+        def multiply_moving(idx):
+            i = UNITS[idx][1]
+            for bp in range(2):
+                acc = psum.tile([P, 2, ROWS], F32, tag="acc", bufs=ACC_BANKS, name="accv")
                 for bb in range(2):
-                    b = 2 * bp + bb
-                    for g in range(G):
-                        nc.tensor.matmul_mx(
-                            out=acc[:, bb, :],
-                            lhsT=x_codes[:, g, b * S : (b + 1) * S].bitcast(FP8X4),
-                            lhsT_scale=x_scales[:, g, b * S : (b + 1) * S],
-                            rhs=wc[:, g * 256 : (g + 1) * 256].bitcast(FP8X4),
-                            rhs_scale=ws[:, g * 256 : (g + 1) * 256],
-                            start=(g == 0),
-                            stop=(g == G - 1),
-                        )
-                fin = fins.tile([P, 2, 256], F32, tag="fin", name="finv")
+                    moving_passes(acc[:, bb, :], idx, 2 * bp + bb)
+                fin = fins.tile([P, 2, ROWS], F32, tag="fin", name="finv")
                 nc.vector.tensor_tensor(
                     out=fin[:],
                     in0=acc[:],
-                    in1=bv_b[:, 256 * i : 256 * (i + 1)].unsqueeze(1).to_broadcast([P, 2, 256]),
+                    in1=bv_b[:, ROWS * i : ROWS * (i + 1)].unsqueeze(1).to_broadcast([P, 2, ROWS]),
                     op=ALU.add,
                 )
                 for bb in range(2):
-                    b = 2 * bp + bb
-                    nc.sync.dma_start(
-                        out=out_1[b, 2 * i : 2 * i + 2, :, :].rearrange("h s d -> s h d"),
-                        in_=fin[:, bb, :].rearrange("p (h d) -> p h d", d=HD),
-                    )
+                    store_values(i, 2 * bp + bb, fin[:, bb, :])
 
-        def spread_bv(q):
-            tpb = psum.tile([P, 4, P], F32, tag="tp", bufs=TPB, name="tpb")
-            for mm in range(4):
-                h = 4 * q + mm
-                nc.tensor.transpose(tpb[:, mm, :], bias_t[:, H + h : H + h + 1].to_broadcast([P, P]), ident[:])
-            nc.scalar.copy(out=bv_b[:, 512 * q : 512 * (q + 1)], in_=tpb[:].rearrange("p m r -> p (m r)"))
+        def multiply_moving_one_batch(idx, b):
+            i = UNITS[idx][1]
+            acc = psum.tile([P, ROWS], F32, tag="tp", bufs=TP_BANKS, name="accb")
+            moving_passes(acc[:], idx, b)
+            fin = fins.tile([P, ROWS], F32, tag="fin", name="finb")
+            nc.vector.tensor_tensor(out=fin[:], in0=acc[:], in1=bv_b[:, ROWS * i : ROWS * (i + 1)], op=ALU.add)
+            store_values(i, b, fin[:])
 
-        next_products(PIECES[0], 4 if CHUNK_FIRST else 1)
-        if LATE_CONST:
-            constants()
+        next_products(2)
 
         xg = []
         for gp in range(2):
             xg_t = grp.tile([P, 2, TOK, 4], BF16, tag="grp", name="xg%d" % gp, align_bytes=64)
             xg.append(xg_t)
         for b in range(NB):
-            words = xr[b // 2][:, b % 2, :].bitcast(F32)
+            words = x_rows[b // 2][:, b % 2, :].bitcast(F32)
             for gp in range(2):
-                tp = psum.tile([P, 2, 2, P], F32, tag="tp", bufs=TPB, name="tpx")
+                tp = psum.tile([P, 2, 2, P], F32, tag="tp", bufs=TP_BANKS, name="tpx")
                 for gg in range(2):
                     g = 2 * gp + gg
                     for u in range(2):
-                        nc.tensor.transpose(tp[:, gg, u, :], words[:, 256 * g + u : 256 * (g + 1) : 2], ident[:])
-                dst = xg[gp][:, :, b * P : (b + 1) * P, :].bitcast(F32)
-                if (b, gp) in XVEC:
-                    nc.vector.tensor_copy(out=dst, in_=tp[:].rearrange("p g u c -> p g c u"))
-                else:
-                    nc.scalar.copy(out=dst, in_=tp[:].rearrange("p g u c -> p g c u"))
-            warm(WARM_X if b in WARM_XB else 0)
+                        nc.tensor.transpose(tp[:, gg, u, :], words[:, WORDS * g + u : WORDS * (g + 1) : 2], ident[:])
+                nc.scalar.copy(out=xg[gp][:, :, b * P : (b + 1) * P, :].bitcast(F32), in_=tp[:].rearrange("p g u c -> p g c u"))
+            keep_clock_in_free_bank(1)
         for gp in range(2):
             nc.vector.quantize_mx(
                 out=x_codes[:, 2 * gp : 2 * gp + 2, :].rearrange("p g c -> p (g c)").bitcast(FP8X4),
@@ -427,107 +316,38 @@ def tile_attention_pb_kernel(tc, key_value, wk, bk, wv_bytes, wv_scale, bv, cos,
         turn(0)
         quantise(0)
 
-        cst = const.tile([P, 3, P], F32, name="cst")
-        tpc = psum.tile([P, 4, P], F32, tag="tp", bufs=TPB, name="tpc")
+        tables = const.tile([P, 3, P], F32, name="tables")
+        tpc = psum.tile([P, 4, P], F32, tag="tp", bufs=TP_BANKS, name="tpc")
         nc.tensor.transpose(tpc[:, 0, :], csf[:, 0, :], ident[:])
         nc.tensor.transpose(tpc[:, 1, :], csf[:, 1, :], ident[:])
         nc.tensor.transpose(tpc[:, 2, :], b_f[:], ident[:])
-        nc.scalar.copy(out=cst[:], in_=tpc[:, 0:3, :])
-        bias_t = cst[:, 2, :]
-        cs2 = const.tile([P, 2, NB, S], F32, name="cs2")
-        if BV == "pe" and -1 in BV_AT:
-            spread_bv(BV_AT[-1])
+        nc.scalar.copy(out=tables[:], in_=tpc[:, 0:3, :])
+        bias_cols = tables[:, 2, :]
+        cos_sin = const.tile([P, 2, NB, S], F32, name="cos_sin")
 
-        def multiply(idx):
-            if units[idx][0] == "v":
-                if V_IN_TP:
-                    multiply_v(idx, (0, 1), "tp", TPB)
-                else:
-                    multiply_v(idx, (0, 1))
-            else:
-                multiply_w(idx)
-                pending.append(idx)
-
-        for p in range(n_units // 2 if PAIRED else 0):
-            a = 2 * p
-            b = a + 1
-            for c in range(2):
-                if len(loaded) < n_units:
-                    load_next()
-            if BV_SLOT == p:
+        for j in range(N_UNITS):
+            if len(loaded) < N_UNITS:
+                load(len(loaded))
+            if j == 1:
                 nc.sync.dma_start(out=bv_b[:], in_=bv.partition_broadcast(P))
-            next_products(PAIR_PIECES[0])
-            if PAIR_BACK == "first":
-                back_upto(a - 1)
-            turn(b)
-            if p == 0:
-                nc.scalar.copy(out=cs2[:], in_=cst[:, 0:2, :].unsqueeze(2).to_broadcast([P, 2, NB, S]))
-            quantise(b)
-            if PAIR_BACK == "mid":
-                back_upto(a - 1)
-            next_products(PAIR_PIECES[1])
-            if a + 2 < n_units:
-                turn(a + 2)
-            if PAIR_BACK == "last":
-                back_upto(a - 1)
-            if a + 4 in ORDERED:
-                permute(a + 4)
-            if a + 2 < n_units:
-                quantise(a + 2)
-            multiply(a)
-            if b < n_units - 1:
-                multiply(b)
-            else:
-                tg, nb = ("tp", TPB) if LAST_TP else ("acc", ACB)
-                for step in LAST_ORDER.split():
-                    if step == "back":
-                        back_upto(b)
-                    elif LAST_SPLIT:
-                        multiply_v1(b, 2 * int(step[1]), tg, nb)
-                        multiply_v1(b, 2 * int(step[1]) + 1, tg, nb)
-                    else:
-                        multiply_v(b, (int(step[1]),), tg, nb)
-
-        for j in range(0 if PAIRED else n_units):
-            if len(loaded) < n_units:
-                load_next()
-            if BV_SLOT == j:
-                nc.sync.dma_start(out=bv_b[:], in_=bv.partition_broadcast(P))
-            if HALVES is None:
-                next_products(PIECES[j + 1] if j + 1 < len(PIECES) else 0)
-            else:
-                first_half()
-            if BACK_FIRST and j < n_units - 1:
-                back_upto(j - BACK)
-            if j + 1 < n_units:
+            next_products(1)
+            if j + 1 < N_UNITS:
                 turn(j + 1)
             if j == 0:
-                nc.scalar.copy(out=cs2[:], in_=cst[:, 0:2, :].unsqueeze(2).to_broadcast([P, 2, NB, S]))
-            if BV == "pe" and j in BV_AT:
-                spread_bv(BV_AT[j])
-            if j + ORDER_AHEAD in ORDERED:
-                permute(j + ORDER_AHEAD)
-            if j + 1 < n_units:
+                nc.scalar.copy(out=cos_sin[:], in_=tables[:, 0:2, :].unsqueeze(2).to_broadcast([P, 2, NB, S]))
+            if j + 2 < N_UNITS and contiguous_words(j + 2):
+                order_words(j + 2)
+            if j + 1 < N_UNITS:
                 quantise(j + 1)
-            if HALVES == "after_q":
-                second_half()
-            if j == n_units - 1:
-                tg, nb = ("tp", TPB) if LAST_TP else ("acc", ACB)
-                for step in LAST_ORDER.split():
-                    if step == "back":
-                        back_upto(j)
-                    elif LAST_SPLIT:
-                        multiply_v1(j, 2 * int(step[1]), tg, nb)
-                        multiply_v1(j, 2 * int(step[1]) + 1, tg, nb)
-                    else:
-                        multiply_v(j, (int(step[1]),), tg, nb)
-            else:
-                if not BACK_FIRST:
-                    back_upto(j - BACK)
-                if units[j][0] == "v":
-                    multiply_v(j, (0, 1))
+            if j < N_UNITS - 1:
+                turn_back_up_to(j - 2)
+                if UNITS[j][0] == "v":
+                    multiply_moving(j)
                 else:
-                    multiply_w(j)
-                    pending.append(j)
-            if HALVES == "after_mul":
-                second_half()
+                    multiply_stationary(j)
+            else:
+                multiply_moving_one_batch(j, 0)
+                multiply_moving_one_batch(j, 1)
+                turn_back_up_to(j)
+                multiply_moving_one_batch(j, 2)
+                multiply_moving_one_batch(j, 3)

@@ -20,7 +20,7 @@ ROWS = 2 * HD
 FLOPS = 2 * TOK * DIM * 2 * H * HD
 
 UNITS = (
-    ("s", 0), ("k", 0), ("k", 1), ("v", 1), ("k", 2), ("v", 2), ("k", 3), ("v", 3),
+    ("s", 0), ("k", 0), ("k", 1), ("v", 1), ("k", 2), ("v", 2), ("k", 3), ("s", 3),
     ("k", 4), ("v", 4), ("k", 5), ("v", 5), ("k", 6), ("v", 6), ("k", 7), ("v", 7),
 )
 N_UNITS = len(UNITS)

@@ -27,7 +27,7 @@ N_UNITS = len(UNITS)
 FIRST_ORDERED = 4
 FIRST_LOADS = (3, 1, 2, 4)
 TP_BANKS, ACC_BANKS, OB_BANKS = 4, 2, 2
-CLOCK_COLUMNS = 256
+CLOCK_COLUMNS = 128
 IDLE_AT_START, IDLE_BEFORE_KEY_VALUE = 6, 3
 FIRST_BETWEEN_PASSES = 3
 BANK = 512

@@ -28,6 +28,7 @@ FIRST_ORDERED = 4
 FIRST_LOADS = (3, 1, 2, 4)
 TP_BANKS, ACC_BANKS, OB_BANKS = 4, 2, 2
 CLOCK_COLUMNS = 128
+IDLE_COLUMNS = 256
 IDLE_AT_START, IDLE_BEFORE_KEY_VALUE = 6, 3
 FIRST_BETWEEN_PASSES = 3
 BANK = 512
@@ -52,15 +53,15 @@ def tile_attention_pb_kernel(tc, key_value, wk, bk, wv_bytes, wv_scale, bv, cos,
         zeros = const.tile([P, TOK], BF16, name="zeros")
         nc.vector.memset(zeros[:], 0.0)
 
-        def keep_clock(bank):
-            nc.tensor.matmul(bank[:, 0:CLOCK_COLUMNS], lhsT=zeros[:, 0:P], rhs=zeros[:, 0:CLOCK_COLUMNS], start=True, stop=True)
+        def keep_clock(bank, columns=CLOCK_COLUMNS):
+            nc.tensor.matmul(bank[:, 0:columns], lhsT=zeros[:, 0:P], rhs=zeros[:, 0:columns], start=True, stop=True)
 
-        def keep_clock_in_free_bank(count):
+        def keep_clock_in_free_bank(count, columns=CLOCK_COLUMNS):
             bank = psum.tile([P, TOK], F32, tag="acc", bufs=ACC_BANKS, name="idle")
             for c in range(count):
-                keep_clock(bank[:])
+                keep_clock(bank[:], columns)
 
-        keep_clock_in_free_bank(IDLE_AT_START)
+        keep_clock_in_free_bank(IDLE_AT_START, IDLE_COLUMNS)
 
         s_raw = const.tile([P, P], F32, name="s_raw")
         nc.gpsimd.memset(s_raw[:], 0.0)
@@ -126,7 +127,7 @@ def tile_attention_pb_kernel(tc, key_value, wk, bk, wv_bytes, wv_scale, bv, cos,
                 m = 4 * q + mm
                 nc.tensor.transpose(tpq[:, mm, :], scol[:, m : m + 1].to_broadcast([P, P]), ident[:])
             nc.vector.tensor_copy(out=scale_b[:, BANK * q : BANK * (q + 1)], in_=tpq[:].rearrange("p m r -> p (m r)"))
-        keep_clock_in_free_bank(IDLE_BEFORE_KEY_VALUE)
+        keep_clock_in_free_bank(IDLE_BEFORE_KEY_VALUE, IDLE_COLUMNS)
 
         x_codes = const.tile([P, G, TOK], U32, name="x_codes", align_bytes=64)
         x_scales = const.tile([P, G, TOK], U8, name="x_scales", align_bytes=64)

@@ -71,10 +71,6 @@ def tile_attention_pb_kernel(tc, key_value, wk, bk, wv_bytes, wv_scale, bv, cos,
         make_identity(nc, ident[:])
         cs_raw = const.tile([P, 2, P], BF16, name="cs_raw")
         nc.sync.dma_start(out=s_raw[0 : DIM // P, :], in_=wv_scale.rearrange("o (m p) -> (o m) p", p=P))
-        nc.sync.dma_start(out=cs_raw[:, 0, :], in_=cos.rearrange("a b s d -> (a b s) d"))
-        nc.sync.dma_start(out=cs_raw[:, 1, :], in_=sin.rearrange("a b s d -> (a b s) d"))
-        nc.sync.dma_start(out=b_raw[0:H, :], in_=bk.rearrange("(h d) -> h d", d=HD))
-        nc.sync.dma_start(out=b_raw[H : 2 * H, :], in_=bv.rearrange("(h d) -> h d", d=HD))
 
         scale_b = const.tile([P, DIM], F32, name="scale_b")
         bv_b = const.tile([P, H * HD], BF16, name="bv_b")
@@ -97,13 +93,25 @@ def tile_attention_pb_kernel(tc, key_value, wk, bk, wv_bytes, wv_scale, bv, cos,
                 wv_bytes_in[idx] = wvy
             loaded.append(idx)
 
-        load(0)
+        first_bytes = vby.tile([P, 2, DIM], U8, tag="vby", name="wvy0")
+        wv_bytes_in[0] = first_bytes
+        loaded.append(0)
+
+        def load_first_bytes(r):
+            nc.sync.dma_start(out=first_bytes[:, r, :], in_=wv_bytes[r * P : (r + 1) * P, :])
+
         x_rows = []
         for j in range(2):
             x_t = raw.tile([P, 2, DIM], BF16, tag="raw", name="xr%d" % j)
             x_rows.append(x_t)
         for b in range(NB):
             nc.sync.dma_start(out=x_rows[b // 2][:, b % 2, :], in_=key_value[b])
+            if b < 2:
+                load_first_bytes(b)
+        nc.sync.dma_start(out=cs_raw[:, 0, :], in_=cos.rearrange("a b s d -> (a b s) d"))
+        nc.sync.dma_start(out=cs_raw[:, 1, :], in_=sin.rearrange("a b s d -> (a b s) d"))
+        nc.sync.dma_start(out=b_raw[0:H, :], in_=bk.rearrange("(h d) -> h d", d=HD))
+        nc.sync.dma_start(out=b_raw[H : 2 * H, :], in_=bv.rearrange("(h d) -> h d", d=HD))
         for idx in FIRST_LOADS:
             load(idx)
 
@@ -112,11 +120,6 @@ def tile_attention_pb_kernel(tc, key_value, wk, bk, wv_bytes, wv_scale, bv, cos,
         b_f = const.tile([P, P], F32, name="b_f")
         nc.vector.tensor_copy(out=perm[:, 0:64], in_=ident[:, 64:128])
         nc.vector.tensor_copy(out=perm[:, 64:128], in_=ident[:, 0:64])
-        nc.vector.tensor_copy(out=csf[:, 0, :], in_=cs_raw[:, 0, :])
-        nc.vector.tensor_copy(out=csf[:, 1, 0:64], in_=cs_raw[:, 1, 64:128])
-        nc.vector.tensor_scalar(out=csf[:, 1, 64:128], in0=cs_raw[:, 1, 0:64], scalar1=-1.0, scalar2=None, op0=ALU.mult)
-        nc.vector.tensor_copy(out=b_f[:], in_=b_raw[:])
-
         scol = const.tile([P, DIM // P], F32, name="scol")
         tp0 = psum.tile([P, NB, S], F32, tag="tp", bufs=TP_BANKS, name="tp0")
         nc.tensor.transpose(tp0[:, 0, :], s_raw[:], ident[:])
@@ -126,7 +129,7 @@ def tile_attention_pb_kernel(tc, key_value, wk, bk, wv_bytes, wv_scale, bv, cos,
             for mm in range(4):
                 m = 4 * q + mm
                 nc.tensor.transpose(tpq[:, mm, :], scol[:, m : m + 1].to_broadcast([P, P]), ident[:])
-            nc.vector.tensor_copy(out=scale_b[:, BANK * q : BANK * (q + 1)], in_=tpq[:].rearrange("p m r -> p (m r)"))
+            (nc.vector.tensor_copy if q % 2 == 0 else nc.scalar.copy)(out=scale_b[:, BANK * q : BANK * (q + 1)], in_=tpq[:].rearrange("p m r -> p (m r)"))
         keep_clock_in_free_bank(IDLE_BEFORE_KEY_VALUE, IDLE_COLUMNS)
 
         x_codes = const.tile([P, G, TOK], U32, name="x_codes", align_bytes=64)
@@ -293,6 +296,11 @@ def tile_attention_pb_kernel(tc, key_value, wk, bk, wv_bytes, wv_scale, bv, cos,
 
         next_products(2)
 
+        nc.vector.tensor_copy(out=csf[:, 0, :], in_=cs_raw[:, 0, :])
+        nc.vector.tensor_copy(out=csf[:, 1, 0:64], in_=cs_raw[:, 1, 64:128])
+        nc.vector.tensor_scalar(out=csf[:, 1, 64:128], in0=cs_raw[:, 1, 0:64], scalar1=-1.0, scalar2=None, op0=ALU.mult)
+        nc.vector.tensor_copy(out=b_f[:], in_=b_raw[:])
+
         xg = []
         for gp in range(2):
             xg_t = grp.tile([P, 2, TOK, 4], BF16, tag="grp", name="xg%d" % gp, align_bytes=64)
@@ -334,7 +342,7 @@ def tile_attention_pb_kernel(tc, key_value, wk, bk, wv_bytes, wv_scale, bv, cos,
             next_products(1)
             if j + 1 < N_UNITS:
                 turn(j + 1)
-            if j == 0:
+            if j == 1:
                 nc.scalar.copy(out=cos_sin[:], in_=tables[:, 0:2, :].unsqueeze(2).to_broadcast([P, 2, NB, S]))
             if j + 2 < N_UNITS and contiguous_words(j + 2):
                 order_words(j + 2)

@@ -296,11 +296,6 @@ def tile_attention_pb_kernel(tc, key_value, wk, bk, wv_bytes, wv_scale, bv, cos,
 
         next_products(2)
 
-        nc.vector.tensor_copy(out=csf[:, 0, :], in_=cs_raw[:, 0, :])
-        nc.vector.tensor_copy(out=csf[:, 1, 0:64], in_=cs_raw[:, 1, 64:128])
-        nc.vector.tensor_scalar(out=csf[:, 1, 64:128], in0=cs_raw[:, 1, 0:64], scalar1=-1.0, scalar2=None, op0=ALU.mult)
-        nc.vector.tensor_copy(out=b_f[:], in_=b_raw[:])
-
         xg = []
         for gp in range(2):
             xg_t = grp.tile([P, 2, TOK, 4], BF16, tag="grp", name="xg%d" % gp, align_bytes=64)
@@ -322,17 +317,26 @@ def tile_attention_pb_kernel(tc, key_value, wk, bk, wv_bytes, wv_scale, bv, cos,
                 in_=xg[gp][:].rearrange("p g c t -> p (g c t)"),
             )
 
+        nc.vector.tensor_copy(out=csf[:, 0, :], in_=cs_raw[:, 0, :])
+        nc.vector.tensor_copy(out=csf[:, 1, 0:64], in_=cs_raw[:, 1, 64:128])
+        nc.vector.tensor_scalar(out=csf[:, 1, 64:128], in0=cs_raw[:, 1, 0:64], scalar1=-1.0, scalar2=None, op0=ALU.mult)
+        nc.vector.tensor_copy(out=b_f[:], in_=b_raw[:])
+
         turn(0)
         quantise(0)
 
         tables = const.tile([P, 3, P], F32, name="tables")
-        tpc = psum.tile([P, 4, P], F32, tag="tp", bufs=TP_BANKS, name="tpc")
-        nc.tensor.transpose(tpc[:, 0, :], csf[:, 0, :], ident[:])
-        nc.tensor.transpose(tpc[:, 1, :], csf[:, 1, :], ident[:])
-        nc.tensor.transpose(tpc[:, 2, :], b_f[:], ident[:])
-        nc.scalar.copy(out=tables[:], in_=tpc[:, 0:3, :])
+
+        def turn_tables():
+            tpc = psum.tile([P, 4, P], F32, tag="tp", bufs=TP_BANKS, name="tpc")
+            nc.tensor.transpose(tpc[:, 0, :], csf[:, 0, :], ident[:])
+            nc.tensor.transpose(tpc[:, 1, :], csf[:, 1, :], ident[:])
+            nc.tensor.transpose(tpc[:, 2, :], b_f[:], ident[:])
+            nc.scalar.copy(out=tables[:], in_=tpc[:, 0:3, :])
+
         bias_cols = tables[:, 2, :]
         cos_sin = const.tile([P, 2, NB, S], F32, name="cos_sin")
+
 
         for j in range(N_UNITS):
             if len(loaded) < N_UNITS:
@@ -342,6 +346,8 @@ def tile_attention_pb_kernel(tc, key_value, wk, bk, wv_bytes, wv_scale, bv, cos,
             next_products(1)
             if j + 1 < N_UNITS:
                 turn(j + 1)
+            if j == 0:
+                turn_tables()
             if j == 1:
                 nc.scalar.copy(out=cos_sin[:], in_=tables[:, 0:2, :].unsqueeze(2).to_broadcast([P, 2, NB, S]))
             if j + 2 < N_UNITS and contiguous_words(j + 2):

@@ -29,7 +29,7 @@ FIRST_LOADS = (3, 1, 2, 4)
 TP_BANKS, ACC_BANKS, OB_BANKS = 4, 2, 2
 CLOCK_COLUMNS = 128
 IDLE_COLUMNS = 256
-IDLE_AT_START, IDLE_BEFORE_KEY_VALUE = 6, 3
+IDLE_AT_START, IDLE_BEFORE_KEY_VALUE = 5, 0
 FIRST_BETWEEN_PASSES = 3
 BANK = 512
 WORDS = 256
@@ -50,7 +50,7 @@ def tile_attention_pb_kernel(tc, key_value, wk, bk, wv_bytes, wv_scale, bv, cos,
         psum = ctx.enter_context(tc.psum_pool(name="psum", bufs=2))
         ctx.enter_context(tc.manual_schedule())
 
-        zeros = const.tile([P, TOK], BF16, name="zeros")
+        zeros = const.tile([P, IDLE_COLUMNS], BF16, name="zeros")
         nc.vector.memset(zeros[:], 0.0)
 
         def keep_clock(bank, columns=CLOCK_COLUMNS):
@@ -145,7 +145,10 @@ def tile_attention_pb_kernel(tc, key_value, wk, bk, wv_bytes, wv_scale, bv, cos,
             if r == 0:
                 wvb = vbf.tile([P, 2, DIM], BF16, tag="vbf", name="wvb%d" % idx)
                 wv_rows[idx] = wvb
-            nc.vector.tensor_tensor(out=wv_rows[idx][:, r, :], in0=wv_bytes_in[idx][:, r, :].bitcast(FP8), in1=scale_b[:], op=ALU.mult)
+            pieces = 2 if (idx, r) == (0, 0) else 1
+            for c in range(pieces):
+                cols = slice(c * DIM // pieces, (c + 1) * DIM // pieces)
+                nc.vector.tensor_tensor(out=wv_rows[idx][:, r, cols], in0=wv_bytes_in[idx][:, r, cols].bitcast(FP8), in1=scale_b[:, cols], op=ALU.mult)
 
         row_tiles = []
         for idx in range(N_UNITS):

@@ -29,7 +29,7 @@ FIRST_LOADS = (3, 1, 2, 4)
 TP_BANKS, ACC_BANKS, OB_BANKS = 4, 2, 2
 CLOCK_COLUMNS = 128
 IDLE_COLUMNS = 256
-IDLE_AT_START, IDLE_BEFORE_KEY_VALUE = 5, 0
+IDLE_AT_START, IDLE_BEFORE_KEY_VALUE = 6, 0
 FIRST_BETWEEN_PASSES = 3
 BANK = 512
 WORDS = 256

from contextlib import ExitStack

import concourse.mybir as mybir
from concourse.masks import make_identity

F32 = mybir.dt.float32
BF16 = mybir.dt.bfloat16
U32 = mybir.dt.uint32
U8 = mybir.dt.uint8
FP8 = mybir.dt.float8_e4m3fn
FP8X4 = mybir.dt.float8_e4m3fn_x4
ALU = mybir.AluOpType
ACT = mybir.ActivationFunctionType

NB, S, DIM, H, HD = 4, 128, 2048, 16, 128
P = 128
G = DIM // 512
TOK = NB * S
ROWS = 2 * HD
FLOPS = 2 * TOK * DIM * 2 * H * HD

UNITS = (
    ("s", 0), ("k", 0), ("k", 1), ("v", 1), ("k", 2), ("v", 2), ("k", 3), ("s", 3),
    ("k", 4), ("v", 4), ("k", 5), ("v", 5), ("k", 6), ("v", 6), ("k", 7), ("v", 7),
)
N_UNITS = len(UNITS)
FIRST_ORDERED = 4
FIRST_LOADS = (3, 1, 2, 4)
TP_BANKS, ACC_BANKS, OB_BANKS = 4, 2, 2
CLOCK_COLUMNS = 128
IDLE_COLUMNS = 256
IDLE_AT_START, IDLE_BEFORE_KEY_VALUE = 6, 0
FIRST_BETWEEN_PASSES = 3
BANK = 512
WORDS = 256


def tile_attention_pb_kernel(tc, key_value, wk, bk, wv_bytes, wv_scale, bv, cos, sin, out_0, out_1):
    nc = tc.nc
    with ExitStack() as ctx:
        const = ctx.enter_context(tc.tile_pool(name="const", bufs=1))
        raw = ctx.enter_context(tc.tile_pool(name="raw", bufs=5))
        vby = ctx.enter_context(tc.tile_pool(name="vby", bufs=4))
        vbf = ctx.enter_context(tc.tile_pool(name="vbf", bufs=4))
        prm = ctx.enter_context(tc.tile_pool(name="prm", bufs=3))
        grp = ctx.enter_context(tc.tile_pool(name="grp", bufs=3))
        cod = ctx.enter_context(tc.tile_pool(name="cod", bufs=3))
        rot = ctx.enter_context(tc.tile_pool(name="rot", bufs=4))
        fins = ctx.enter_context(tc.tile_pool(name="fins", bufs=6))
        psum = ctx.enter_context(tc.psum_pool(name="psum", bufs=2))
        ctx.enter_context(tc.manual_schedule())

        zeros = const.tile([P, IDLE_COLUMNS], BF16, name="zeros")
        nc.vector.memset(zeros[:], 0.0)

        def keep_clock(bank, columns=CLOCK_COLUMNS):
            nc.tensor.matmul(bank[:, 0:columns], lhsT=zeros[:, 0:P], rhs=zeros[:, 0:columns], start=True, stop=True)

        def keep_clock_in_free_bank(count, columns=CLOCK_COLUMNS):
            bank = psum.tile([P, TOK], F32, tag="acc", bufs=ACC_BANKS, name="idle")
            for c in range(count):
                keep_clock(bank[:], columns)

        keep_clock_in_free_bank(IDLE_AT_START, IDLE_COLUMNS)

        s_raw = const.tile([P, P], F32, name="s_raw")
        nc.gpsimd.memset(s_raw[:], 0.0)
        b_raw = const.tile([P, P], BF16, name="b_raw")
        nc.gpsimd.memset(b_raw[:], 0.0)
        ident = const.tile([P, P], F32, name="ident")
        make_identity(nc, ident[:])
        cs_raw = const.tile([P, 2, P], BF16, name="cs_raw")
        nc.sync.dma_start(out=s_raw[0 : DIM // P, :], in_=wv_scale.rearrange("o (m p) -> (o m) p", p=P))

        scale_b = const.tile([P, DIM], F32, name="scale_b")
        bv_b = const.tile([P, H * HD], BF16, name="bv_b")

        wk_rows = {}
        wv_bytes_in = {}
        wv_rows = {}
        loaded = []

        def load(idx):
            kind, i = UNITS[idx]
            span = slice(ROWS * i, ROWS * (i + 1))
            if kind == "k":
                wkr = raw.tile([P, 2, DIM], BF16, tag="raw", name="wkr%d" % i)
                nc.sync.dma_start(out=wkr[:], in_=wk[span, :].rearrange("(r p) k -> p r k", p=P))
                wk_rows[idx] = wkr
            else:
                wvy = vby.tile([P, 2, DIM], U8, tag="vby", name="wvy%d" % i)
                nc.sync.dma_start(out=wvy[:], in_=wv_bytes[span, :].rearrange("(r p) k -> p r k", p=P))
                wv_bytes_in[idx] = wvy
            loaded.append(idx)

        first_bytes = vby.tile([P, 2, DIM], U8, tag="vby", name="wvy0")
        wv_bytes_in[0] = first_bytes
        loaded.append(0)

        def load_first_bytes(r):
            nc.sync.dma_start(out=first_bytes[:, r, :], in_=wv_bytes[r * P : (r + 1) * P, :])

        x_rows = []
        for j in range(2):
            x_t = raw.tile([P, 2, DIM], BF16, tag="raw", name="xr%d" % j)
            x_rows.append(x_t)
        for b in range(NB):
            nc.sync.dma_start(out=x_rows[b // 2][:, b % 2, :], in_=key_value[b])
            if b < 2:
                load_first_bytes(b)
        nc.sync.dma_start(out=cs_raw[:, 0, :], in_=cos.rearrange("a b s d -> (a b s) d"))
        nc.sync.dma_start(out=cs_raw[:, 1, :], in_=sin.rearrange("a b s d -> (a b s) d"))
        nc.sync.dma_start(out=b_raw[0:H, :], in_=bk.rearrange("(h d) -> h d", d=HD))
        nc.sync.dma_start(out=b_raw[H : 2 * H, :], in_=bv.rearrange("(h d) -> h d", d=HD))
        for idx in FIRST_LOADS:
            load(idx)

        perm = const.tile([P, P], F32, name="perm")
        csf = const.tile([P, 2, P], F32, name="csf")
        b_f = const.tile([P, P], F32, name="b_f")
        nc.vector.tensor_copy(out=perm[:, 0:64], in_=ident[:, 64:128])
        nc.vector.tensor_copy(out=perm[:, 64:128], in_=ident[:, 0:64])
        scol = const.tile([P, DIM // P], F32, name="scol")
        tp0 = psum.tile([P, NB, S], F32, tag="tp", bufs=TP_BANKS, name="tp0")
        nc.tensor.transpose(tp0[:, 0, :], s_raw[:], ident[:])
        nc.scalar.copy(out=scol[:], in_=tp0[:, 0, 0 : DIM // P])
        for q in range(4):
            tpq = psum.tile([P, 4, P], F32, tag="tp", bufs=TP_BANKS, name="tpq")
            for mm in range(4):
                m = 4 * q + mm
                nc.tensor.transpose(tpq[:, mm, :], scol[:, m : m + 1].to_broadcast([P, P]), ident[:])
            (nc.vector.tensor_copy if q % 2 == 0 else nc.scalar.copy)(out=scale_b[:, BANK * q : BANK * (q + 1)], in_=tpq[:].rearrange("p m r -> p (m r)"))
        keep_clock_in_free_bank(IDLE_BEFORE_KEY_VALUE, IDLE_COLUMNS)

        x_codes = const.tile([P, G, TOK], U32, name="x_codes", align_bytes=64)
        x_scales = const.tile([P, G, TOK], U8, name="x_scales", align_bytes=64)

        ordered = {}
        groups = {}
        codes = {}
        by_feature = {}
        to_turn_back = []

        def product(idx, r):
            if r == 0:
                wvb = vbf.tile([P, 2, DIM], BF16, tag="vbf", name="wvb%d" % idx)
                wv_rows[idx] = wvb
            pieces = 2 if (idx, r) == (0, 0) else 1
            for c in range(pieces):
                cols = slice(c * DIM // pieces, (c + 1) * DIM // pieces)
                nc.vector.tensor_tensor(out=wv_rows[idx][:, r, cols], in0=wv_bytes_in[idx][:, r, cols].bitcast(FP8), in1=scale_b[:, cols], op=ALU.mult)

        row_tiles = []
        for idx in range(N_UNITS):
            if UNITS[idx][0] != "k":
                row_tiles.append((idx, 0))
                row_tiles.append((idx, 1))

        def next_products(count):
            for c in range(count):
                if len(row_tiles) > 0:
                    idx, r = row_tiles.pop(0)
                    product(idx, r)

        def contiguous_words(idx):
            return UNITS[idx][0] == "k" and idx >= FIRST_ORDERED

        def order_words(idx):
            wkp = prm.tile([P, 2, G, 2, P], F32, tag="prm", name="wkp%d" % idx)
            ordered[idx] = wkp
            for r in range(2):
                nc.scalar.copy(out=wkp[:, r, :, :, :], in_=wk_rows[idx][:, r, :].bitcast(F32).rearrange("p (g j u) -> p g u j", g=G, u=2))

        def turn(idx):
            wg = grp.tile([P, G, ROWS, 4], BF16, tag="grp", name="wg%d" % idx, align_bytes=64)
            groups[idx] = wg
            for r in range(2):
                for gp in range(2):
                    tp = psum.tile([P, 2, 2, P], F32, tag="tp", bufs=TP_BANKS, name="tpw")
                    if idx >= FIRST_BETWEEN_PASSES and not contiguous_words(idx) and (r, gp) == (1, 0):
                        keep_clock(tp[:].rearrange("p g u c -> p (g u c)"))
                    for gg in range(2):
                        g = 2 * gp + gg
                        for u in range(2):
                            if contiguous_words(idx):
                                nc.tensor.transpose(tp[:, gg, u, :], ordered[idx][:, r, g, u, :], ident[:])
                            else:
                                rows = wk_rows[idx] if UNITS[idx][0] == "k" else wv_rows[idx]
                                words = rows[:, r, :].bitcast(F32)
                                nc.tensor.transpose(tp[:, gg, u, :], words[:, WORDS * g + u : WORDS * (g + 1) : 2], ident[:])
                    nc.scalar.copy(out=wg[:, 2 * gp : 2 * gp + 2, r * P : (r + 1) * P, :].bitcast(F32), in_=tp[:].rearrange("p g u c -> p g c u"))
                if idx < FIRST_BETWEEN_PASSES:
                    keep_clock_in_free_bank(1)

        def quantise(idx):
            wc = cod.tile([P, G * ROWS], U32, tag="wc", name="wc%d" % idx, align_bytes=64)
            ws = cod.tile([P, G * ROWS], U8, tag="ws", name="ws%d" % idx, align_bytes=64)
            nc.vector.quantize_mx(out=wc[:].bitcast(FP8X4), scales=ws[:], in_=groups[idx][:].rearrange("p g c t -> p (g c t)"))
            codes[idx] = (wc, ws)

        def multiply_stationary(idx):
            kind, i = UNITS[idx]
            wc, ws = codes[idx]
            pair = []
            for r in range(2):
                h = 2 * i + r
                acc = psum.tile([P, TOK], F32, tag="acc", bufs=ACC_BANKS, name="acck")
                for g in range(G):
                    cols = slice(g * ROWS + r * P, g * ROWS + (r + 1) * P)
                    nc.tensor.matmul_mx(
                        out=acc[:],
                        lhsT=wc[:, cols].bitcast(FP8X4),
                        lhsT_scale=ws[:, cols],
                        rhs=x_codes[:, g, :].bitcast(FP8X4),
                        rhs_scale=x_scales[:, g, :],
                        start=(g == 0),
                        stop=(g == G - 1),
                    )
                if kind == "k":
                    res = rot.tile([P, 2, TOK], F32, tag="rab", name="rab%d" % h)
                    nc.vector.scalar_tensor_tensor(
                        out=res[:],
                        in0=acc[:].unsqueeze(1).to_broadcast([P, 2, TOK]),
                        scalar=bias_cols[:, h : h + 1],
                        in1=cos_sin[:].rearrange("p c b s -> p c (b s)"),
                        op0=ALU.add,
                        op1=ALU.mult,
                    )
                else:
                    res = rot.tile([P, TOK], F32, tag="rab", name="vb%d" % h)
                    nc.scalar.activation(out=res[:], in_=acc[:], func=ACT.Identity, bias=bias_cols[:, H + h : H + h + 1], scale=1.0)
                pair.append(res)
            by_feature[idx] = pair
            to_turn_back.append(idx)

        def turn_back(idx):
            kind, i = UNITS[idx]
            for r in range(2):
                h = 2 * i + r
                res = by_feature[idx][r]
                ob = psum.tile([P, NB, HD], F32, tag="ob", bufs=OB_BANKS, name="ob")
                for b in range(NB):
                    cols = slice(b * S, (b + 1) * S)
                    if kind == "k":
                        nc.tensor.matmul(ob[:, b, :], lhsT=res[:, 0, cols], rhs=ident[:], is_transpose=True, start=True, stop=False)
                        nc.tensor.matmul(ob[:, b, :], lhsT=res[:, 1, cols], rhs=perm[:], is_transpose=True, start=False, stop=True)
                    else:
                        nc.tensor.transpose(ob[:, b, :], res[:, cols], ident[:])
                fin = fins.tile([P, NB, HD], F32, tag="fin", name="fink")
                nc.scalar.copy(out=fin[:], in_=ob[:])
                dst = out_0 if kind == "k" else out_1
                nc.sync.dma_start(out=dst[:, h, :, :].rearrange("b s d -> s b d"), in_=fin[:])

        def turn_back_up_to(last):
            for idx in list(to_turn_back):
                if idx <= last:
                    to_turn_back.remove(idx)
                    turn_back(idx)

        def moving_passes(acc, idx, b):
            wc, ws = codes[idx]
            for g in range(G):
                nc.tensor.matmul_mx(
                    out=acc,
                    lhsT=x_codes[:, g, b * S : (b + 1) * S].bitcast(FP8X4),
                    lhsT_scale=x_scales[:, g, b * S : (b + 1) * S],
                    rhs=wc[:, g * ROWS : (g + 1) * ROWS].bitcast(FP8X4),
                    rhs_scale=ws[:, g * ROWS : (g + 1) * ROWS],
                    start=(g == 0),
                    stop=(g == G - 1),
                )

        def store_values(i, b, fin):
            nc.sync.dma_start(out=out_1[b, 2 * i : 2 * i + 2, :, :].rearrange("h s d -> s h d"), in_=fin.rearrange("p (h d) -> p h d", d=HD))

        def multiply_moving(idx):
            i = UNITS[idx][1]
            for bp in range(2):
                acc = psum.tile([P, 2, ROWS], F32, tag="acc", bufs=ACC_BANKS, name="accv")
                for bb in range(2):
                    moving_passes(acc[:, bb, :], idx, 2 * bp + bb)
                fin = fins.tile([P, 2, ROWS], F32, tag="fin", name="finv")
                nc.vector.tensor_tensor(
                    out=fin[:],
                    in0=acc[:],
                    in1=bv_b[:, ROWS * i : ROWS * (i + 1)].unsqueeze(1).to_broadcast([P, 2, ROWS]),
                    op=ALU.add,
                )
                for bb in range(2):
                    store_values(i, 2 * bp + bb, fin[:, bb, :])

        def multiply_moving_one_batch(idx, b):
            i = UNITS[idx][1]
            acc = psum.tile([P, ROWS], F32, tag="tp", bufs=TP_BANKS, name="accb")
            moving_passes(acc[:], idx, b)
            fin = fins.tile([P, ROWS], F32, tag="fin", name="finb")
            nc.vector.tensor_tensor(out=fin[:], in0=acc[:], in1=bv_b[:, ROWS * i : ROWS * (i + 1)], op=ALU.add)
            store_values(i, b, fin[:])

        next_products(2)

        xg = []
        for gp in range(2):
            xg_t = grp.tile([P, 2, TOK, 4], BF16, tag="grp", name="xg%d" % gp, align_bytes=64)
            xg.append(xg_t)
        for b in range(NB):
            words = x_rows[b // 2][:, b % 2, :].bitcast(F32)
            for gp in range(2):
                tp = psum.tile([P, 2, 2, P], F32, tag="tp", bufs=TP_BANKS, name="tpx")
                for gg in range(2):
                    g = 2 * gp + gg
                    for u in range(2):
                        nc.tensor.transpose(tp[:, gg, u, :], words[:, WORDS * g + u : WORDS * (g + 1) : 2], ident[:])
                nc.scalar.copy(out=xg[gp][:, :, b * P : (b + 1) * P, :].bitcast(F32), in_=tp[:].rearrange("p g u c -> p g c u"))
            keep_clock_in_free_bank(1)
        for gp in range(2):
            nc.vector.quantize_mx(
                out=x_codes[:, 2 * gp : 2 * gp + 2, :].rearrange("p g c -> p (g c)").bitcast(FP8X4),
                scales=x_scales[:, 2 * gp : 2 * gp + 2, :].rearrange("p g c -> p (g c)"),
                in_=xg[gp][:].rearrange("p g c t -> p (g c t)"),
            )

        nc.vector.tensor_copy(out=csf[:, 0, :], in_=cs_raw[:, 0, :])
        nc.vector.tensor_copy(out=csf[:, 1, 0:64], in_=cs_raw[:, 1, 64:128])
        nc.vector.tensor_scalar(out=csf[:, 1, 64:128], in0=cs_raw[:, 1, 0:64], scalar1=-1.0, scalar2=None, op0=ALU.mult)
        nc.vector.tensor_copy(out=b_f[:], in_=b_raw[:])

        turn(0)
        quantise(0)

        tables = const.tile([P, 3, P], F32, name="tables")

        def turn_tables():
            tpc = psum.tile([P, 4, P], F32, tag="tp", bufs=TP_BANKS, name="tpc")
            nc.tensor.transpose(tpc[:, 0, :], csf[:, 0, :], ident[:])
            nc.tensor.transpose(tpc[:, 1, :], csf[:, 1, :], ident[:])
            nc.tensor.transpose(tpc[:, 2, :], b_f[:], ident[:])
            nc.scalar.copy(out=tables[:], in_=tpc[:, 0:3, :])

        bias_cols = tables[:, 2, :]
        cos_sin = const.tile([P, 2, NB, S], F32, name="cos_sin")


        for j in range(N_UNITS):
            if len(loaded) < N_UNITS:
                load(len(loaded))
            if j == 1:
                nc.sync.dma_start(out=bv_b[:], in_=bv.partition_broadcast(P))
            next_products(1)
            if j + 1 < N_UNITS:
                turn(j + 1)
            if j == 0:
                turn_tables()
            if j == 1:
                nc.scalar.copy(out=cos_sin[:], in_=tables[:, 0:2, :].unsqueeze(2).to_broadcast([P, 2, NB, S]))
            if j + 2 < N_UNITS and contiguous_words(j + 2):
                order_words(j + 2)
            if j + 1 < N_UNITS:
                quantise(j + 1)
            if j < N_UNITS - 1:
                turn_back_up_to(j - 2)
                if UNITS[j][0] == "v":
                    multiply_moving(j)
                else:
                    multiply_stationary(j)
            else:
                multiply_moving_one_batch(j, 0)
                multiply_moving_one_batch(j, 1)
                turn_back_up_to(j)
                multiply_moving_one_batch(j, 2)
                multiply_moving_one_batch(j, 3)
